import numpy as np
import ml_dtypes


def mxq(x, axis, fmt="e4m3"):
    dtype, down = {"e4m3": (ml_dtypes.float8_e4m3fn, 7), "e5m2": (ml_dtypes.float8_e5m2, 14)}[fmt]
    v = np.moveaxis(np.asarray(x, np.float32).astype(ml_dtypes.bfloat16).astype(np.float64), axis, -1)
    blocks = v.reshape(v.shape[:-1] + (-1, 32))
    amax = np.abs(blocks).max(-1, keepdims=True)
    byte = np.maximum(np.where(amax > 0, np.frexp(amax)[1] - 1 + 127, 0) - down, 1)
    scale = np.exp2(byte - 127.0)
    codes = (blocks / scale).astype(np.float32).astype(dtype).astype(np.float64)
    return np.moveaxis((codes * scale).reshape(v.shape), -1, axis)


WIDE = False


def mx_kscale(k):
    if not WIDE:
        return np.ones(k)
    levels = np.array([10, -10, 5, -5, 0])
    a = np.random.permutation(np.resize(levels, k // 512 * 4)).reshape(k // 512, 4)
    idx = np.arange(k)
    return np.exp2(a[idx // 512, idx % 128 // 32])


BF16 = ml_dtypes.bfloat16


def bf(x):
    return np.asarray(x, np.float32).astype(BF16)


def f64(x):
    return np.asarray(x).astype(np.float64)


B, I, U = 256, 1024, 1024
QR = True


def hard_sigmoid(v):
    return np.clip(0.2 * v + 0.5, 0.0, 1.0)


def rec_mm(a, w):
    if QR:
        return mxq(a, 1, "e4m3") @ mxq(w, 0, "e4m3")
    return a @ w


def setup_inputs():
    s = mx_kscale(I)
    t = mx_kscale(U) if QR else np.ones(U)
    r = mx_kscale(U) if QR else np.ones(U)
    bias = np.random.standard_normal(4 * U) * 0.1
    bias[U:2 * U] += 1.0
    return {"inputs": bf(np.random.standard_normal((B, I)) * s),
            "h_tm1": bf(np.random.standard_normal((B, U)) * t),
            "c_tm1": bf(np.random.standard_normal((B, U))),
            "z_tm1": bf(np.random.standard_normal((B, U)) * r),
            "kernel": bf(np.random.standard_normal((I, 4 * U)) / np.sqrt(I) / s[:, None]),
            "recurrent_kernel": bf(np.random.standard_normal((U, 4 * U)) / np.sqrt(U) / t[:, None]),
            "recurrent_latent": bf(np.random.standard_normal((U, 4 * U)) / np.sqrt(U) / r[:, None]),
            "bias": bf(bias)}


def reference(inputs, h_tm1, c_tm1, z_tm1, kernel, recurrent_kernel, recurrent_latent, bias):
    x = (mxq(f64(inputs), 1, "e4m3") @ mxq(f64(kernel), 0, "e4m3")) + rec_mm(f64(h_tm1), f64(recurrent_kernel)) + rec_mm(f64(z_tm1), f64(recurrent_latent)) + f64(bias)
    x_i, x_f, x_c, x_o = np.split(x, 4, axis=1)
    i = hard_sigmoid(x_i)
    f = hard_sigmoid(x_f)
    c = f * f64(c_tm1) + i * np.tanh(x_c)
    o = hard_sigmoid(x_o)
    h = o * np.tanh(c)
    return h

@@ -1,0 +1,191 @@
+from contextlib import ExitStack
+
+import concourse.mybir as mybir
+from concourse.masks import make_identity
+
+FLOPS = 2 * 256 * 3072 * 4096
+
+FP8X4 = mybir.dt.float8_e4m3fn_x4
+BF16 = mybir.dt.bfloat16
+F32 = mybir.dt.float32
+U32 = mybir.dt.uint32
+U8 = mybir.dt.uint8
+ACT = mybir.ActivationFunctionType
+ALU = mybir.AluOpType
+
+P = 128
+B = 256
+U = 1024
+NJ = 8
+PASSES = 6
+CV = 544
+GATE_ORDER = (2, 0, 1, 3)
+RAW_BUFS = 8
+
+
+def tile_vlstmcell_kernel(tc, inputs, h_tm1, c_tm1, z_tm1, kernel, recurrent_kernel,
+                                     recurrent_latent, bias, out):
+    nc = tc.nc
+    weights = (kernel, recurrent_kernel, recurrent_latent)
+    with ExitStack() as ctx:
+        const = ctx.enter_context(tc.tile_pool(name="const", bufs=1))
+        rawp = ctx.enter_context(tc.tile_pool(name="rawp", bufs=RAW_BUFS))
+        grpp = ctx.enter_context(tc.tile_pool(name="grpp", bufs=3))
+        codp = ctx.enter_context(tc.tile_pool(name="codp", bufs=8))
+        tmpp = ctx.enter_context(tc.tile_pool(name="tmpp", bufs=3))
+        psum = ctx.enter_context(tc.psum_pool(name="psum", bufs=1))
+
+        ident_f = const.tile([P, P], F32)
+        make_identity(nc, ident_f[:])
+        ident_b = const.tile([P, P], BF16)
+        make_identity(nc, ident_b[:])
+        warm = const.tile([P, 1], F32)
+        nc.vector.memset(warm[:], 0.0)
+        warm2 = const.tile([P, 1], F32)
+        nc.scalar.activation(out=warm2[:], in_=warm[:], func=ACT.Tanh)
+
+        bias_rows = const.tile([P, P], BF16)
+        nc.vector.memset(bias_rows[:], 0.0)
+        nc.scalar.dma_start(out=bias_rows[0:32, :], in_=bias.rearrange("(r c) -> r c", c=P))
+
+        units = [(g, c) for g in GATE_ORDER for c in range(PASSES)]
+        raws = {}
+
+        def load_unit(i):
+            g, c = units[i]
+            raw = rawp.tile([P, 4, U], BF16, name="raw")
+            src = weights[c // 2][512 * (c % 2):512 * (c % 2) + 512, :].rearrange("(p j) n -> p j n", j=4)
+            nc.sync.dma_start(out=raw[:], in_=src[:, :, U * g:U * g + U])
+            raws[i] = raw
+
+        def load_act(src, nm):
+            t = const.tile([P, 2 * U], BF16, name=nm)
+            nc.sync.dma_start(out=t[:].rearrange("p (m k) -> p m k", m=2),
+                              in_=src.rearrange("(m p) k -> p m k", p=P))
+            return t
+
+        x_sb = load_act(inputs, "x_sb")
+        load_unit(0)
+        h_sb = load_act(h_tm1, "h_sb")
+        z_sb = load_act(z_tm1, "z_sb")
+        load_unit(1)
+        load_unit(2)
+        c_sb = load_act(c_tm1, "c_sb")
+        for i in range(3, RAW_BUFS):
+            load_unit(i)
+
+        b_ps = psum.tile([P, P], BF16, tag="b6", name="b_ps")
+        nc.tensor.transpose(b_ps[:], bias_rows[:], ident_b[:])
+        b32 = const.tile([P, 32], F32)
+        nc.vector.tensor_copy(out=b32[:], in_=b_ps[:, 0:32])
+        hb = const.tile([P, 32], F32)
+        nc.vector.tensor_scalar(out=hb[:], in0=b32[:], scalar1=0.2, scalar2=0.5, op0=ALU.mult, op1=ALU.add)
+
+        a_codes = const.tile([P, PASSES * B], U32, align_bytes=64)
+        a_scales = const.tile([P, PASSES * B], U8, align_bytes=64)
+        for s, a_sb in enumerate((x_sb, h_sb, z_sb)):
+            a32 = a_sb[:].bitcast(F32)
+            ga = const.tile([P, 2 * 4 * B], BF16, align_bytes=64, name="ga%d" % s)
+            ga32 = ga[:].bitcast(F32)
+            for gl in range(2):
+                xt = psum.tile([P, 2, B], F32, tag="b%d" % (2 * s + gl), name="xt")
+                for m in range(2):
+                    for u in range(2):
+                        w0 = 512 * m + 256 * gl
+                        nc.tensor.transpose(xt[:, u, P * m:P * m + P], a32[:, w0 + u:w0 + 256:2], ident_f[:])
+                dst = ga32[:, 512 * gl:512 * gl + 512].rearrange("p (b u) -> p b u", u=2)
+                srcv = xt[:].rearrange("p u b -> p b u")
+                if gl == 0:
+                    nc.vector.tensor_copy(out=dst, in_=srcv)
+                else:
+                    nc.scalar.copy(out=dst, in_=srcv)
+            nc.vector.quantize_mx(out=a_codes[:, 512 * s:512 * s + 512].bitcast(FP8X4),
+                                  scales=a_scales[:, 512 * s:512 * s + 512], in_=ga[:])
+
+        cT = const.tile([P, NJ, B], BF16)
+        for hh in range(2):
+            c_ps = psum.tile([P, 4, B], BF16, tag="b%d" % (6 + hh), name="c_ps")
+            for jj in range(4):
+                for m in range(2):
+                    col = U * m + P * (4 * hh + jj)
+                    nc.tensor.transpose(c_ps[:, jj, P * m:P * m + P], c_sb[:, col:col + P], ident_b[:])
+            if hh == 0:
+                nc.vector.tensor_copy(out=cT[:, 0:4, :], in_=c_ps[:])
+            else:
+                nc.scalar.copy(out=cT[:, 4:8, :], in_=c_ps[:])
+
+        state = const.tile([P, NJ, B], F32)
+        o_sb = const.tile([P, 2, U], F32)
+        grouped = {}
+        acc = {}
+
+        def regroup(i):
+            raw = raws[i]
+            grp = grpp.tile([P, U, 4], BF16, align_bytes=64, name="grp")
+            nc.vector.tensor_copy(out=grp[:, 0:CV, :].rearrange("p (c i) t -> p c t i", i=4),
+                                  in_=raw[:, :, 0:CV].rearrange("p t (c i) -> p c t i", i=4))
+            nc.scalar.copy(out=grp[:, CV:U, :].rearrange("p (c i) t -> p c t i", i=4),
+                           in_=raw[:, :, CV:U].rearrange("p t (c i) -> p c t i", i=4))
+            grouped[i] = grp
+
+        def flat(ap):
+            return ap.rearrange("p j b -> p (j b)")
+
+        def finish(i):
+            g, c = units[i]
+            codes = codp.tile([P, U], U32, align_bytes=64, name="codes")
+            scales = codp.tile([P, U], U8, align_bytes=64, name="scales")
+            nc.vector.quantize_mx(out=codes[:].bitcast(FP8X4), scales=scales[:],
+                                  in_=grouped[i][:].rearrange("p w j -> p (w j)"))
+            for j in range(NJ):
+                if c == 0:
+                    acc[j] = psum.tile([P, B], F32, tag="b%d" % j, name="acc")
+                nc.tensor.matmul_mx(out=acc[j][:],
+                                    lhsT=codes[:, P * j:P * j + P].bitcast(FP8X4),
+                                    lhsT_scale=scales[:, P * j:P * j + P],
+                                    rhs=a_codes[:, B * c:B * c + B].bitcast(FP8X4),
+                                    rhs_scale=a_scales[:, B * c:B * c + B],
+                                    start=(c == 0), stop=(c == PASSES - 1))
+            if c != PASSES - 1:
+                return
+            if g == 2:
+                for j in range(NJ):
+                    nc.scalar.activation(out=state[:, j, :], in_=acc[j][:], func=ACT.Tanh,
+                                         bias=b32[:, 8 * g + j:8 * g + j + 1], scale=1.0)
+                return
+            for hh in range(2):
+                js = slice(4 * hh, 4 * hh + 4)
+                tmp = tmpp.tile([P, 4, B], F32, name="tmp")
+                for jj in range(4):
+                    j = 4 * hh + jj
+                    nc.scalar.activation(out=tmp[:, jj, :], in_=acc[j][:], func=ACT.Relu,
+                                         bias=hb[:, 8 * g + j:8 * g + j + 1], scale=0.2)
+                st = flat(state[:, js, :])
+                if g == 1:
+                    nc.vector.scalar_tensor_tensor(out=flat(tmp[:]), in0=flat(tmp[:]), scalar=1.0,
+                                                   in1=flat(cT[:, js, :]), op0=ALU.min, op1=ALU.mult)
+                    nc.vector.tensor_tensor(out=st, in0=st, in1=flat(tmp[:]), op=ALU.add)
+                    nc.scalar.activation(out=st, in_=st, func=ACT.Tanh)
+                else:
+                    nc.vector.scalar_tensor_tensor(out=st, in0=flat(tmp[:]), scalar=1.0, in1=st,
+                                                   op0=ALU.min, op1=ALU.mult)
+                if g == 3:
+                    for m in range(2):
+                        hp = psum.tile([P, 512], F32, tag="b%d" % (2 * hh + m), name="hp")
+                        for jj in range(4):
+                            nc.tensor.transpose(hp[:, P * jj:P * jj + P],
+                                                state[:, 4 * hh + jj, P * m:P * m + P], ident_f[:])
+                        dst = o_sb[:, m, 512 * hh:512 * hh + 512]
+                        if m == 0:
+                            nc.vector.tensor_copy(out=dst, in_=hp[:])
+                        else:
+                            nc.scalar.copy(out=dst, in_=hp[:])
+                        nc.sync.dma_start(out=out[P * m:P * m + P, 512 * hh:512 * hh + 512], in_=dst)
+
+        for i in range(len(units)):
+            regroup(i)
+            if i + RAW_BUFS < len(units):
+                load_unit(i + RAW_BUFS)
+            if i >= 1:
+                finish(i - 1)
+        finish(len(units) - 1)

@@ -18,9 +18,19 @@ B = 256
 U = 1024
 NJ = 8
 PASSES = 6
-CV = 544
 GATE_ORDER = (2, 0, 1, 3)
+N_UNITS = 24
+N_STREAM = 22
+BW = 256
 RAW_BUFS = 8
+GRP_BUFS = 3
+COD_BUFS = 8
+
+V_RG = 0.000428
+S_RG = 0.000836
+T_Q = 0.91
+COST = {"acopy": 0.49, "aquant": 0.46, "gate": 1.1, "mix1": 0.91, "mix2": 1.83, "tanh_c": 0.91,
+        "ctrans": 0.0, "ccopy": 0.49}
 
 
 def tile_vlstmcell_kernel(tc, inputs, h_tm1, c_tm1, z_tm1, kernel, recurrent_kernel,
@@ -30,10 +40,38 @@ def tile_vlstmcell_kernel(tc, inputs, h_tm1, c_tm1, z_tm1, kernel, recurrent_ker
     with ExitStack() as ctx:
         const = ctx.enter_context(tc.tile_pool(name="const", bufs=1))
         rawp = ctx.enter_context(tc.tile_pool(name="rawp", bufs=RAW_BUFS))
-        grpp = ctx.enter_context(tc.tile_pool(name="grpp", bufs=3))
-        codp = ctx.enter_context(tc.tile_pool(name="codp", bufs=8))
+        grpp = ctx.enter_context(tc.tile_pool(name="grpp", bufs=GRP_BUFS))
+        codp = ctx.enter_context(tc.tile_pool(name="codp", bufs=COD_BUFS))
         tmpp = ctx.enter_context(tc.tile_pool(name="tmpp", bufs=3))
         psum = ctx.enter_context(tc.psum_pool(name="psum", bufs=1))
+        ctx.enter_context(tc.manual_schedule())
+
+        slots = N_STREAM
+        s_work = [[] for k in range(slots + 8)]
+        v_work = [[] for k in range(slots + 8)]
+        s_work[0] += [("acopy", 1, 0), ("acopy", 1, 1)]
+        v_work[1] += [("aquant", 1, 0)]
+        s_work[1] += [("acopy", 2, 0), ("acopy", 2, 1)]
+        v_work[2] += [("aquant", 2, 0)]
+        for gi in range(3):
+            e = PASSES * gi + PASSES - 1
+            for hh in range(2):
+                s_work[e + 2 + hh].append(("gate", gi, hh))
+                if gi >= 1:
+                    v_work[e + 3 + hh].append(("mix%d" % gi, gi, hh))
+                if gi == 2:
+                    s_work[e + 4 + hh].append(("tanh_c", gi, hh))
+        s_work[8].append(("ctrans", 0, 0))
+        s_work[9] += [("ccopy", 0, 0), ("ccopy", 0, 1)]
+
+        def split(s):
+            s_fix = sum(COST[w[0]] for w in s_work[s])
+            v_fix = sum(COST[w[0]] for w in v_work[s]) + (T_Q if s >= 1 else 0.0)
+            cv = (s_fix + 4 * U * S_RG - v_fix) / (4 * (V_RG + S_RG))
+            cv = 8 * int(round(cv / 8))
+            if cv > U - 64:
+                return U
+            return max(cv, 64)
 
         ident_f = const.tile([P, P], F32)
         make_identity(nc, ident_f[:])
@@ -42,11 +80,11 @@ def tile_vlstmcell_kernel(tc, inputs, h_tm1, c_tm1, z_tm1, kernel, recurrent_ker
         warm = const.tile([P, 1], F32)
         nc.vector.memset(warm[:], 0.0)
         warm2 = const.tile([P, 1], F32)
-        nc.scalar.activation(out=warm2[:], in_=warm[:], func=ACT.Tanh)
-
         bias_rows = const.tile([P, P], BF16)
-        nc.vector.memset(bias_rows[:], 0.0)
-        nc.scalar.dma_start(out=bias_rows[0:32, :], in_=bias.rearrange("(r c) -> r c", c=P))
+        nc.sync.dma_start(out=bias_rows[0:32, :], in_=bias.rearrange("(r c) -> r c", c=P))
+        nc.vector.memset(bias_rows[32:64, :], 0.0)
+        nc.vector.memset(bias_rows[64:128, :], 0.0)
+        nc.scalar.activation(out=warm2[:], in_=warm[:], func=ACT.Tanh)
 
         units = [(g, c) for g in GATE_ORDER for c in range(PASSES)]
         raws = {}
@@ -67,14 +105,16 @@ def tile_vlstmcell_kernel(tc, inputs, h_tm1, c_tm1, z_tm1, kernel, recurrent_ker
         x_sb = load_act(inputs, "x_sb")
         load_unit(0)
         h_sb = load_act(h_tm1, "h_sb")
-        z_sb = load_act(z_tm1, "z_sb")
         load_unit(1)
-        load_unit(2)
-        c_sb = load_act(c_tm1, "c_sb")
-        for i in range(3, RAW_BUFS):
+        z_sb = load_act(z_tm1, "z_sb")
+        for i in range(2, 6):
             load_unit(i)
+        c_sb = load_act(c_tm1, "c_sb")
+        for i in range(6, RAW_BUFS):
+            load_unit(i)
+        acts = (x_sb, h_sb, z_sb)
 
-        b_ps = psum.tile([P, P], BF16, tag="b6", name="b_ps")
+        b_ps = psum.tile([P, P], BF16, tag="b7", name="b_ps")
         nc.tensor.transpose(b_ps[:], bias_rows[:], ident_b[:])
         b32 = const.tile([P, 32], F32)
         nc.vector.tensor_copy(out=b32[:], in_=b_ps[:, 0:32])
@@ -83,109 +123,226 @@ def tile_vlstmcell_kernel(tc, inputs, h_tm1, c_tm1, z_tm1, kernel, recurrent_ker
 
         a_codes = const.tile([P, PASSES * B], U32, align_bytes=64)
         a_scales = const.tile([P, PASSES * B], U8, align_bytes=64)
-        for s, a_sb in enumerate((x_sb, h_sb, z_sb)):
-            a32 = a_sb[:].bitcast(F32)
-            ga = const.tile([P, 2 * 4 * B], BF16, align_bytes=64, name="ga%d" % s)
-            ga32 = ga[:].bitcast(F32)
-            for gl in range(2):
-                xt = psum.tile([P, 2, B], F32, tag="b%d" % (2 * s + gl), name="xt")
-                for m in range(2):
-                    for u in range(2):
-                        w0 = 512 * m + 256 * gl
-                        nc.tensor.transpose(xt[:, u, P * m:P * m + P], a32[:, w0 + u:w0 + 256:2], ident_f[:])
-                dst = ga32[:, 512 * gl:512 * gl + 512].rearrange("p (b u) -> p b u", u=2)
-                srcv = xt[:].rearrange("p u b -> p b u")
-                if gl == 0:
-                    nc.vector.tensor_copy(out=dst, in_=srcv)
-                else:
-                    nc.scalar.copy(out=dst, in_=srcv)
-            nc.vector.quantize_mx(out=a_codes[:, 512 * s:512 * s + 512].bitcast(FP8X4),
-                                  scales=a_scales[:, 512 * s:512 * s + 512], in_=ga[:])
-
+        ga = [const.tile([P, 2 * 4 * B], BF16, align_bytes=64, name="ga%d" % s) for s in range(3)]
         cT = const.tile([P, NJ, B], BF16)
-        for hh in range(2):
-            c_ps = psum.tile([P, 4, B], BF16, tag="b%d" % (6 + hh), name="c_ps")
-            for jj in range(4):
-                for m in range(2):
-                    col = U * m + P * (4 * hh + jj)
-                    nc.tensor.transpose(c_ps[:, jj, P * m:P * m + P], c_sb[:, col:col + P], ident_b[:])
-            if hh == 0:
-                nc.vector.tensor_copy(out=cT[:, 0:4, :], in_=c_ps[:])
-            else:
-                nc.scalar.copy(out=cT[:, 4:8, :], in_=c_ps[:])
-
         state = const.tile([P, NJ, B], F32)
         o_sb = const.tile([P, 2, U], F32)
+        bank_free = [False] * 6 + [True, True]
+        a_ready = [False] * 3
         grouped = {}
+        coded = {}
         acc = {}
-
-        def regroup(i):
-            raw = raws[i]
-            grp = grpp.tile([P, U, 4], BF16, align_bytes=64, name="grp")
-            nc.vector.tensor_copy(out=grp[:, 0:CV, :].rearrange("p (c i) t -> p c t i", i=4),
-                                  in_=raw[:, :, 0:CV].rearrange("p t (c i) -> p c t i", i=4))
-            nc.scalar.copy(out=grp[:, CV:U, :].rearrange("p (c i) t -> p c t i", i=4),
-                           in_=raw[:, :, CV:U].rearrange("p t (c i) -> p c t i", i=4))
-            grouped[i] = grp
+        tmp_of = {}
+        c_ps = {}
+        pe_queue = [(i, j) for i in range(N_STREAM) for j in range(NJ)]
+        pe_head = [0]
 
         def flat(ap):
             return ap.rearrange("p j b -> p (j b)")
 
-        def finish(i):
-            g, c = units[i]
+        def act_copy(s, gl, eng):
+            a32 = acts[s][:].bitcast(F32)
+            xt = psum.tile([P, 2, B], F32, tag="b%d" % (2 * s + gl), name="xt")
+            for m in range(2):
+                for u in range(2):
+                    w0 = 512 * m + 256 * gl
+                    nc.tensor.transpose(xt[:, u, P * m:P * m + P], a32[:, w0 + u:w0 + 256:2], ident_f[:])
+            dst = ga[s][:].bitcast(F32)[:, 512 * gl:512 * gl + 512].rearrange("p (b u) -> p b u", u=2)
+            srcv = xt[:].rearrange("p u b -> p b u")
+            if eng == "v":
+                nc.vector.tensor_copy(out=dst, in_=srcv)
+            else:
+                nc.scalar.copy(out=dst, in_=srcv)
+            bank_free[2 * s + gl] = True
+
+        def act_quant(s):
+            nc.vector.quantize_mx(out=a_codes[:, 512 * s:512 * s + 512].bitcast(FP8X4),
+                                  scales=a_scales[:, 512 * s:512 * s + 512], in_=ga[s][:])
+            a_ready[s] = True
+
+        def regroup(i, cv):
+            raw = raws[i]
+            grp = grpp.tile([P, U, 4], BF16, align_bytes=64, name="grp")
+            nc.vector.tensor_copy(out=grp[:, 0:cv, :].rearrange("p (c i) t -> p c t i", i=4),
+                                  in_=raw[:, :, 0:cv].rearrange("p t (c i) -> p c t i", i=4))
+            if cv < U:
+                nc.scalar.copy(out=grp[:, cv:U, :].rearrange("p (c i) t -> p c t i", i=4),
+                               in_=raw[:, :, cv:U].rearrange("p t (c i) -> p c t i", i=4))
+            grouped[i] = grp
+
+        def quantise(i):
             codes = codp.tile([P, U], U32, align_bytes=64, name="codes")
             scales = codp.tile([P, U], U8, align_bytes=64, name="scales")
             nc.vector.quantize_mx(out=codes[:].bitcast(FP8X4), scales=scales[:],
                                   in_=grouped[i][:].rearrange("p w j -> p (w j)"))
-            for j in range(NJ):
+            coded[i] = (codes, scales)
+
+        def flush_pe():
+            while pe_head[0] < len(pe_queue):
+                i, j = pe_queue[pe_head[0]]
+                c = i % PASSES
+                if i not in coded or not a_ready[c // 2]:
+                    return
                 if c == 0:
+                    if not bank_free[j]:
+                        return
                     acc[j] = psum.tile([P, B], F32, tag="b%d" % j, name="acc")
+                    bank_free[j] = False
+                codes, scales = coded[i]
                 nc.tensor.matmul_mx(out=acc[j][:],
                                     lhsT=codes[:, P * j:P * j + P].bitcast(FP8X4),
                                     lhsT_scale=scales[:, P * j:P * j + P],
                                     rhs=a_codes[:, B * c:B * c + B].bitcast(FP8X4),
                                     rhs_scale=a_scales[:, B * c:B * c + B],
                                     start=(c == 0), stop=(c == PASSES - 1))
-            if c != PASSES - 1:
-                return
-            if g == 2:
-                for j in range(NJ):
+                pe_head[0] += 1
+
+        def gate_act(gi, hh):
+            g = GATE_ORDER[gi]
+            if gi > 0:
+                tmp_of[(gi, hh)] = tmpp.tile([P, 4, B], F32, name="tmp")
+            for jj in range(4):
+                j = 4 * hh + jj
+                if gi == 0:
                     nc.scalar.activation(out=state[:, j, :], in_=acc[j][:], func=ACT.Tanh,
                                          bias=b32[:, 8 * g + j:8 * g + j + 1], scale=1.0)
-                return
-            for hh in range(2):
-                js = slice(4 * hh, 4 * hh + 4)
-                tmp = tmpp.tile([P, 4, B], F32, name="tmp")
-                for jj in range(4):
-                    j = 4 * hh + jj
-                    nc.scalar.activation(out=tmp[:, jj, :], in_=acc[j][:], func=ACT.Relu,
-                                         bias=hb[:, 8 * g + j:8 * g + j + 1], scale=0.2)
-                st = flat(state[:, js, :])
-                if g == 1:
-                    nc.vector.scalar_tensor_tensor(out=flat(tmp[:]), in0=flat(tmp[:]), scalar=1.0,
-                                                   in1=flat(cT[:, js, :]), op0=ALU.min, op1=ALU.mult)
-                    nc.vector.tensor_tensor(out=st, in0=st, in1=flat(tmp[:]), op=ALU.add)
-                    nc.scalar.activation(out=st, in_=st, func=ACT.Tanh)
                 else:
-                    nc.vector.scalar_tensor_tensor(out=st, in0=flat(tmp[:]), scalar=1.0, in1=st,
-                                                   op0=ALU.min, op1=ALU.mult)
-                if g == 3:
-                    for m in range(2):
-                        hp = psum.tile([P, 512], F32, tag="b%d" % (2 * hh + m), name="hp")
-                        for jj in range(4):
-                            nc.tensor.transpose(hp[:, P * jj:P * jj + P],
-                                                state[:, 4 * hh + jj, P * m:P * m + P], ident_f[:])
-                        dst = o_sb[:, m, 512 * hh:512 * hh + 512]
-                        if m == 0:
-                            nc.vector.tensor_copy(out=dst, in_=hp[:])
-                        else:
-                            nc.scalar.copy(out=dst, in_=hp[:])
-                        nc.sync.dma_start(out=out[P * m:P * m + P, 512 * hh:512 * hh + 512], in_=dst)
+                    nc.scalar.activation(out=tmp_of[(gi, hh)][:, jj, :], in_=acc[j][:], func=ACT.Relu,
+                                         bias=hb[:, 8 * g + j:8 * g + j + 1], scale=0.2)
+                bank_free[j] = True
 
-        for i in range(len(units)):
-            regroup(i)
-            if i + RAW_BUFS < len(units):
-                load_unit(i + RAW_BUFS)
-            if i >= 1:
-                finish(i - 1)
-        finish(len(units) - 1)
+        def mix(gi, hh):
+            js = slice(4 * hh, 4 * hh + 4)
+            tmp = tmp_of[(gi, hh)]
+            st = flat(state[:, js, :])
+            if gi == 2:
+                nc.vector.scalar_tensor_tensor(out=flat(tmp[:]), in0=flat(tmp[:]), scalar=1.0,
+                                               in1=flat(cT[:, js, :]), op0=ALU.min, op1=ALU.mult)
+                nc.vector.tensor_tensor(out=st, in0=st, in1=flat(tmp[:]), op=ALU.add)
+            else:
+                nc.vector.scalar_tensor_tensor(out=st, in0=flat(tmp[:]), scalar=1.0, in1=st,
+                                               op0=ALU.min, op1=ALU.mult)
+
+        def do(w):
+            kind, a, b = w
+            if kind == "acopy":
+                act_copy(a, b, "s")
+            elif kind == "aquant":
+                act_quant(a)
+            elif kind == "gate":
+                gate_act(a, b)
+            elif kind == "mix1" or kind == "mix2":
+                mix(a, b)
+            elif kind == "tanh_c":
+                st = flat(state[:, 4 * b:4 * b + 4, :])
+                nc.scalar.activation(out=st, in_=st, func=ACT.Tanh)
+            elif kind == "ctrans":
+                for hh in range(2):
+                    c_ps[hh] = psum.tile([P, 4, B], BF16, tag="b%d" % (6 + hh), name="c_ps")
+                    bank_free[6 + hh] = False
+                    for jj in range(4):
+                        for m in range(2):
+                            col = U * m + P * (4 * hh + jj)
+                            nc.tensor.transpose(c_ps[hh][:, jj, P * m:P * m + P], c_sb[:, col:col + P], ident_b[:])
+            elif kind == "ccopy":
+                nc.scalar.copy(out=cT[:, 4 * b:4 * b + 4, :], in_=c_ps[b][:])
+                bank_free[6 + b] = True
+
+        act_copy(0, 0, "v")
+        act_copy(0, 1, "s")
+        act_quant(0)
+
+        next_load = [RAW_BUFS]
+        for s in range(slots):
+            regroup(s, split(s))
+            if next_load[0] < N_UNITS:
+                load_unit(next_load[0])
+                next_load[0] += 1
+            if s >= 1:
+                quantise(s - 1)
+            for w in s_work[s]:
+                do(w)
+            for w in v_work[s]:
+                do(w)
+            flush_pe()
+
+        out_v = out.rearrange("(m p) u -> p m u", p=P)
+        blk = {}
+
+        def block_regroup(q):
+            grp = grpp.tile([P, U, 4], BF16, align_bytes=64, name="grp")
+            cols = slice(BW * q, BW * q + BW)
+            nc.vector.tensor_copy(out=grp[:, 0:BW, :].rearrange("p (c i) t -> p c t i", i=4),
+                                  in_=raws[N_STREAM][:, :, cols].rearrange("p t (c i) -> p c t i", i=4))
+            nc.scalar.copy(out=grp[:, BW:2 * BW, :].rearrange("p (c i) t -> p c t i", i=4),
+                           in_=raws[N_STREAM + 1][:, :, cols].rearrange("p t (c i) -> p c t i", i=4))
+            blk[q] = grp
+
+        def block_multiply(q):
+            codes = codp.tile([P, U], U32, align_bytes=64, name="codes")
+            scales = codp.tile([P, U], U8, align_bytes=64, name="scales")
+            nc.vector.quantize_mx(out=codes[:, 0:2 * BW].bitcast(FP8X4), scales=scales[:, 0:2 * BW],
+                                  in_=blk[q][:, 0:2 * BW, :].rearrange("p w j -> p (w j)"))
+            for cc in range(2):
+                c = PASSES - 2 + cc
+                for jj in range(2):
+                    w0 = BW * cc + P * jj
+                    nc.tensor.matmul_mx(out=acc[2 * q + jj][:],
+                                        lhsT=codes[:, w0:w0 + P].bitcast(FP8X4),
+                                        lhsT_scale=scales[:, w0:w0 + P],
+                                        rhs=a_codes[:, B * c:B * c + B].bitcast(FP8X4),
+                                        rhs_scale=a_scales[:, B * c:B * c + B],
+                                        start=False, stop=(cc == 1))
+
+        def block_act(q):
+            g = GATE_ORDER[3]
+            tmp_of[q] = tmpp.tile([P, 4, B], F32, name="tmp")
+            for jj in range(2):
+                j = 2 * q + jj
+                nc.scalar.activation(out=tmp_of[q][:, jj, :], in_=acc[j][:], func=ACT.Relu,
+                                     bias=hb[:, 8 * g + j:8 * g + j + 1], scale=0.2)
+
+        hp = {}
+
+        def block_mix(q):
+            st = flat(state[:, 2 * q:2 * q + 2, :])
+            nc.vector.scalar_tensor_tensor(out=st, in0=flat(tmp_of[q][:, 0:2, :]), scalar=1.0, in1=st,
+                                           op0=ALU.min, op1=ALU.mult)
+            hp[q] = psum.tile([P, 2, BW], F32, tag="b%d" % (2 * q), name="hp")
+            for m in range(2):
+                for jj in range(2):
+                    nc.tensor.transpose(hp[q][:, m, P * jj:P * jj + P],
+                                        state[:, 2 * q + jj, P * m:P * m + P], ident_f[:])
+
+        def block_store(q, eng):
+            dst = o_sb[:, :, BW * q:BW * q + BW]
+            if eng == "v":
+                nc.vector.tensor_copy(out=dst, in_=hp[q][:])
+            else:
+                nc.scalar.copy(out=dst, in_=hp[q][:])
+            nc.sync.dma_start(out=out_v[:, :, BW * q:BW * q + BW], in_=dst)
+
+        block_regroup(0)
+        quantise(N_STREAM - 1)
+        for w in s_work[N_STREAM]:
+            do(w)
+        flush_pe()
+        block_regroup(1)
+        block_multiply(0)
+        block_regroup(2)
+        block_multiply(1)
+        block_act(0)
+        block_regroup(3)
+        block_multiply(2)
+        block_act(1)
+        block_mix(0)
+        block_multiply(3)
+        block_act(2)
+        block_mix(1)
+        block_store(0, "s")
+        block_act(3)
+        block_mix(2)
+        block_store(1, "s")
+        block_mix(3)
+        block_store(2, "s")
+        block_store(3, "v")

@@ -29,8 +29,12 @@ COD_BUFS = 8
 V_RG = 0.000428
 S_RG = 0.000836
 T_Q = 0.91
-COST = {"acopy": 0.49, "aquant": 0.46, "gate": 1.1, "mix1": 0.91, "mix2": 1.83, "tanh_c": 0.91,
-        "ctrans": 0.0, "ccopy": 0.49}
+COST = {"acopy": 0.49, "aquant": 0.46, "gate": 1.1, "mix": 0.91, "tanh_c": 0.91,
+        "ctrans": 0.0, "ccopy": 0.49, "sum_c": 0.0}
+
+
+def bank_of(gi, j):
+    return j if gi < 3 else (j + 4) % NJ
 
 
 def tile_vlstmcell_kernel(tc, inputs, h_tm1, c_tm1, z_tm1, kernel, recurrent_kernel,
@@ -49,6 +53,7 @@ def tile_vlstmcell_kernel(tc, inputs, h_tm1, c_tm1, z_tm1, kernel, recurrent_ker
         slots = N_STREAM
         s_work = [[] for k in range(slots + 8)]
         v_work = [[] for k in range(slots + 8)]
+        p_work = [[] for k in range(slots + 8)]
         s_work[0] += [("acopy", 1, 0), ("acopy", 1, 1)]
         v_work[1] += [("aquant", 1, 0)]
         s_work[1] += [("acopy", 2, 0), ("acopy", 2, 1)]
@@ -58,8 +63,9 @@ def tile_vlstmcell_kernel(tc, inputs, h_tm1, c_tm1, z_tm1, kernel, recurrent_ker
             for hh in range(2):
                 s_work[e + 2 + hh].append(("gate", gi, hh))
                 if gi >= 1:
-                    v_work[e + 3 + hh].append(("mix%d" % gi, gi, hh))
+                    v_work[e + 3 + hh].append(("mix", gi, hh))
                 if gi == 2:
+                    p_work[e + 3 + hh].append(("sum_c", gi, hh))
                     s_work[e + 4 + hh].append(("tanh_c", gi, hh))
         s_work[8].append(("ctrans", 0, 0))
         s_work[9] += [("ccopy", 0, 0), ("ccopy", 0, 1)]
@@ -126,7 +132,7 @@ def tile_vlstmcell_kernel(tc, inputs, h_tm1, c_tm1, z_tm1, kernel, recurrent_ker
         ga = [const.tile([P, 2 * 4 * B], BF16, align_bytes=64, name="ga%d" % s) for s in range(3)]
         cT = const.tile([P, NJ, B], BF16)
         state = const.tile([P, NJ, B], F32)
-        o_sb = const.tile([P, 2, U], F32)
+        th = const.tile([P, 2, U], F32)
         bank_free = [False] * 6 + [True, True]
         a_ready = [False] * 3
         grouped = {}
@@ -134,8 +140,12 @@ def tile_vlstmcell_kernel(tc, inputs, h_tm1, c_tm1, z_tm1, kernel, recurrent_ker
         acc = {}
         tmp_of = {}
         c_ps = {}
-        pe_queue = [(i, j) for i in range(N_STREAM) for j in range(NJ)]
-        pe_head = [0]
+        ct = {}
+        pe_queue = [[] for b in range(NJ)]
+        for i in range(N_STREAM):
+            for j in range(NJ):
+                pe_queue[bank_of(i // PASSES, j)].append((i, j))
+        pe_head = [0] * NJ
 
         def flat(ap):
             return ap.rearrange("p j b -> p (j b)")
@@ -177,25 +187,31 @@ def tile_vlstmcell_kernel(tc, inputs, h_tm1, c_tm1, z_tm1, kernel, recurrent_ker
                                   in_=grouped[i][:].rearrange("p w j -> p (w j)"))
             coded[i] = (codes, scales)
 
+        def ready(b):
+            if pe_head[b] >= len(pe_queue[b]):
+                return False
+            i, j = pe_queue[b][pe_head[b]]
+            c = i % PASSES
+            return i in coded and a_ready[c // 2] and (c != 0 or bank_free[b])
+
         def flush_pe():
-            while pe_head[0] < len(pe_queue):
-                i, j = pe_queue[pe_head[0]]
-                c = i % PASSES
-                if i not in coded or not a_ready[c // 2]:
+            while True:
+                cand = [pe_queue[b][pe_head[b]] + (b,) for b in range(NJ) if ready(b)]
+                if not cand:
                     return
+                i, j, b = min(cand)
+                gi, c = divmod(i, PASSES)
                 if c == 0:
-                    if not bank_free[j]:
-                        return
-                    acc[j] = psum.tile([P, B], F32, tag="b%d" % j, name="acc")
-                    bank_free[j] = False
+                    acc[(gi, j)] = psum.tile([P, B], F32, tag="b%d" % b, name="acc")
+                    bank_free[b] = False
                 codes, scales = coded[i]
-                nc.tensor.matmul_mx(out=acc[j][:],
+                nc.tensor.matmul_mx(out=acc[(gi, j)][:],
                                     lhsT=codes[:, P * j:P * j + P].bitcast(FP8X4),
                                     lhsT_scale=scales[:, P * j:P * j + P],
                                     rhs=a_codes[:, B * c:B * c + B].bitcast(FP8X4),
                                     rhs_scale=a_scales[:, B * c:B * c + B],
                                     start=(c == 0), stop=(c == PASSES - 1))
-                pe_head[0] += 1
+                pe_head[b] += 1
 
         def gate_act(gi, hh):
             g = GATE_ORDER[gi]
@@ -204,24 +220,38 @@ def tile_vlstmcell_kernel(tc, inputs, h_tm1, c_tm1, z_tm1, kernel, recurrent_ker
             for jj in range(4):
                 j = 4 * hh + jj
                 if gi == 0:
-                    nc.scalar.activation(out=state[:, j, :], in_=acc[j][:], func=ACT.Tanh,
+                    nc.scalar.activation(out=state[:, j, :], in_=acc[(gi, j)][:], func=ACT.Tanh,
                                          bias=b32[:, 8 * g + j:8 * g + j + 1], scale=1.0)
                 else:
-                    nc.scalar.activation(out=tmp_of[(gi, hh)][:, jj, :], in_=acc[j][:], func=ACT.Relu,
+                    nc.scalar.activation(out=tmp_of[(gi, hh)][:, jj, :], in_=acc[(gi, j)][:], func=ACT.Relu,
                                          bias=hb[:, 8 * g + j:8 * g + j + 1], scale=0.2)
-                bank_free[j] = True
+                bank_free[j] = not (gi == 2 and hh == 0)
 
         def mix(gi, hh):
             js = slice(4 * hh, 4 * hh + 4)
             tmp = tmp_of[(gi, hh)]
-            st = flat(state[:, js, :])
             if gi == 2:
                 nc.vector.scalar_tensor_tensor(out=flat(tmp[:]), in0=flat(tmp[:]), scalar=1.0,
                                                in1=flat(cT[:, js, :]), op0=ALU.min, op1=ALU.mult)
-                nc.vector.tensor_tensor(out=st, in0=st, in1=flat(tmp[:]), op=ALU.add)
             else:
+                st = flat(state[:, js, :])
                 nc.vector.scalar_tensor_tensor(out=st, in0=flat(tmp[:]), scalar=1.0, in1=st,
                                                op0=ALU.min, op1=ALU.mult)
+
+        def sum_c(hh):
+            for m in range(2):
+                ct[(hh, m)] = psum.tile([P, 512], F32, tag="b%d" % (2 * hh + m), name="ct")
+                for jj in range(4):
+                    dst = ct[(hh, m)][:, P * jj:P * jj + P]
+                    nc.tensor.matmul(dst, lhsT=state[:, 4 * hh + jj, P * m:P * m + P], rhs=ident_f[:],
+                                     is_transpose=True, start=True, stop=False)
+                    nc.tensor.matmul(dst, lhsT=tmp_of[(2, hh)][:, jj, P * m:P * m + P], rhs=ident_f[:],
+                                     is_transpose=True, start=False, stop=True)
+
+        def tanh_c(hh):
+            for m in range(2):
+                nc.scalar.activation(out=th[:, m, 512 * hh:512 * hh + 512], in_=ct[(hh, m)][:], func=ACT.Tanh)
+                bank_free[2 * hh + m] = True
 
         def do(w):
             kind, a, b = w
@@ -231,11 +261,12 @@ def tile_vlstmcell_kernel(tc, inputs, h_tm1, c_tm1, z_tm1, kernel, recurrent_ker
                 act_quant(a)
             elif kind == "gate":
                 gate_act(a, b)
-            elif kind == "mix1" or kind == "mix2":
+            elif kind == "mix":
                 mix(a, b)
+            elif kind == "sum_c":
+                sum_c(b)
             elif kind == "tanh_c":
-                st = flat(state[:, 4 * b:4 * b + 4, :])
-                nc.scalar.activation(out=st, in_=st, func=ACT.Tanh)
+                tanh_c(b)
             elif kind == "ctrans":
                 for hh in range(2):
                     c_ps[hh] = psum.tile([P, 4, B], BF16, tag="b%d" % (6 + hh), name="c_ps")
@@ -265,9 +296,12 @@ def tile_vlstmcell_kernel(tc, inputs, h_tm1, c_tm1, z_tm1, kernel, recurrent_ker
             for w in v_work[s]:
                 do(w)
             flush_pe()
+            for w in p_work[s]:
+                do(w)
 
         out_v = out.rearrange("(m p) u -> p m u", p=P)
         blk = {}
+        hp = {}
 
         def block_regroup(q):
             grp = grpp.tile([P, U, 4], BF16, align_bytes=64, name="grp")
@@ -287,7 +321,7 @@ def tile_vlstmcell_kernel(tc, inputs, h_tm1, c_tm1, z_tm1, kernel, recurrent_ker
                 c = PASSES - 2 + cc
                 for jj in range(2):
                     w0 = BW * cc + P * jj
-                    nc.tensor.matmul_mx(out=acc[2 * q + jj][:],
+                    nc.tensor.matmul_mx(out=acc[(3, 2 * q + jj)][:],
                                         lhsT=codes[:, w0:w0 + P].bitcast(FP8X4),
                                         lhsT_scale=scales[:, w0:w0 + P],
                                         rhs=a_codes[:, B * c:B * c + B].bitcast(FP8X4),
@@ -296,53 +330,40 @@ def tile_vlstmcell_kernel(tc, inputs, h_tm1, c_tm1, z_tm1, kernel, recurrent_ker
 
         def block_act(q):
             g = GATE_ORDER[3]
-            tmp_of[q] = tmpp.tile([P, 4, B], F32, name="tmp")
+            tmp = tmpp.tile([P, 4, B], F32, name="tmp")
             for jj in range(2):
                 j = 2 * q + jj
-                nc.scalar.activation(out=tmp_of[q][:, jj, :], in_=acc[j][:], func=ACT.Relu,
+                nc.scalar.activation(out=tmp[:, jj, :], in_=acc[(3, j)][:], func=ACT.Relu,
                                      bias=hb[:, 8 * g + j:8 * g + j + 1], scale=0.2)
-
-        hp = {}
-
-        def block_mix(q):
-            st = flat(state[:, 2 * q:2 * q + 2, :])
-            nc.vector.scalar_tensor_tensor(out=st, in0=flat(tmp_of[q][:, 0:2, :]), scalar=1.0, in1=st,
-                                           op0=ALU.min, op1=ALU.mult)
-            hp[q] = psum.tile([P, 2, BW], F32, tag="b%d" % (2 * q), name="hp")
+            hp[q] = psum.tile([P, 2, BW], F32, tag="b%d" % bank_of(3, 2 * q), name="hp")
             for m in range(2):
                 for jj in range(2):
-                    nc.tensor.transpose(hp[q][:, m, P * jj:P * jj + P],
-                                        state[:, 2 * q + jj, P * m:P * m + P], ident_f[:])
+                    nc.tensor.transpose(hp[q][:, m, P * jj:P * jj + P], tmp[:, jj, P * m:P * m + P], ident_f[:])
 
-        def block_store(q, eng):
-            dst = o_sb[:, :, BW * q:BW * q + BW]
-            if eng == "v":
-                nc.vector.tensor_copy(out=dst, in_=hp[q][:])
-            else:
-                nc.scalar.copy(out=dst, in_=hp[q][:])
+        def block_finish(q):
+            dst = th[:, :, BW * q:BW * q + BW]
+            nc.vector.scalar_tensor_tensor(out=dst, in0=hp[q][:], scalar=1.0, in1=dst,
+                                           op0=ALU.min, op1=ALU.mult)
             nc.sync.dma_start(out=out_v[:, :, BW * q:BW * q + BW], in_=dst)
 
         block_regroup(0)
         quantise(N_STREAM - 1)
-        for w in s_work[N_STREAM]:
-            do(w)
         flush_pe()
         block_regroup(1)
         block_multiply(0)
+        for w in s_work[N_STREAM]:
+            do(w)
+        flush_pe()
         block_regroup(2)
         block_multiply(1)
         block_act(0)
         block_regroup(3)
         block_multiply(2)
         block_act(1)
-        block_mix(0)
+        block_finish(0)
         block_multiply(3)
         block_act(2)
-        block_mix(1)
-        block_store(0, "s")
+        block_finish(1)
         block_act(3)
-        block_mix(2)
-        block_store(1, "s")
-        block_mix(3)
-        block_store(2, "s")
-        block_store(3, "v")
+        block_finish(2)
+        block_finish(3)

@@ -25,6 +25,7 @@ BW = 256
 RAW_BUFS = 8
 GRP_BUFS = 3
 COD_BUFS = 8
+C_AFTER = 14
 
 V_RG = 0.000428
 S_RG = 0.000836
@@ -67,8 +68,8 @@ def tile_vlstmcell_kernel(tc, inputs, h_tm1, c_tm1, z_tm1, kernel, recurrent_ker
                 if gi == 2:
                     p_work[e + 3 + hh].append(("sum_c", gi, hh))
                     s_work[e + 4 + hh].append(("tanh_c", gi, hh))
-        s_work[8].append(("ctrans", 0, 0))
-        s_work[9] += [("ccopy", 0, 0), ("ccopy", 0, 1)]
+        s_work[14].append(("ctrans", 0, 0))
+        s_work[15] += [("ccopy", 0, 0), ("ccopy", 0, 1)]
 
         def split(s):
             s_fix = sum(COST[w[0]] for w in s_work[s])
@@ -104,8 +105,7 @@ def tile_vlstmcell_kernel(tc, inputs, h_tm1, c_tm1, z_tm1, kernel, recurrent_ker
 
         def load_act(src, nm):
             t = const.tile([P, 2 * U], BF16, name=nm)
-            nc.sync.dma_start(out=t[:].rearrange("p (m k) -> p m k", m=2),
-                              in_=src.rearrange("(m p) k -> p m k", p=P))
+            nc.sync.dma_start(out=t[:], in_=src.rearrange("(p m) k -> p (m k)", m=2))
             return t
 
         x_sb = load_act(inputs, "x_sb")
@@ -113,12 +113,10 @@ def tile_vlstmcell_kernel(tc, inputs, h_tm1, c_tm1, z_tm1, kernel, recurrent_ker
         h_sb = load_act(h_tm1, "h_sb")
         load_unit(1)
         z_sb = load_act(z_tm1, "z_sb")
-        for i in range(2, 6):
-            load_unit(i)
-        c_sb = load_act(c_tm1, "c_sb")
-        for i in range(6, RAW_BUFS):
+        for i in range(2, RAW_BUFS):
             load_unit(i)
         acts = (x_sb, h_sb, z_sb)
+        c_sb = {}
 
         b_ps = psum.tile([P, P], BF16, tag="b7", name="b_ps")
         nc.tensor.transpose(b_ps[:], bias_rows[:], ident_b[:])
@@ -274,7 +272,7 @@ def tile_vlstmcell_kernel(tc, inputs, h_tm1, c_tm1, z_tm1, kernel, recurrent_ker
                     for jj in range(4):
                         for m in range(2):
                             col = U * m + P * (4 * hh + jj)
-                            nc.tensor.transpose(c_ps[hh][:, jj, P * m:P * m + P], c_sb[:, col:col + P], ident_b[:])
+                            nc.tensor.transpose(c_ps[hh][:, jj, P * m:P * m + P], c_sb[0][:, col:col + P], ident_b[:])
             elif kind == "ccopy":
                 nc.scalar.copy(out=cT[:, 4 * b:4 * b + 4, :], in_=c_ps[b][:])
                 bank_free[6 + b] = True
@@ -288,6 +286,8 @@ def tile_vlstmcell_kernel(tc, inputs, h_tm1, c_tm1, z_tm1, kernel, recurrent_ker
             regroup(s, split(s))
             if next_load[0] < N_UNITS:
                 load_unit(next_load[0])
+                if next_load[0] == C_AFTER:
+                    c_sb[0] = load_act(c_tm1, "c_sb")
                 next_load[0] += 1
             if s >= 1:
                 quantise(s - 1)
@@ -299,7 +299,7 @@ def tile_vlstmcell_kernel(tc, inputs, h_tm1, c_tm1, z_tm1, kernel, recurrent_ker
             for w in p_work[s]:
                 do(w)
 
-        out_v = out.rearrange("(m p) u -> p m u", p=P)
+        out_v = out.rearrange("(p m) u -> p m u", m=2)
         blk = {}
         hp = {}
 

@@ -19,19 +19,19 @@ U = 1024
 NJ = 8
 PASSES = 6
 GATE_ORDER = (2, 0, 1, 3)
-N_UNITS = 24
-N_STREAM = 22
+N_UNITS = 4 * PASSES
+N_STREAM = N_UNITS - 2
 BW = 256
 RAW_BUFS = 8
 GRP_BUFS = 3
 COD_BUFS = 8
+TMP_BUFS = 3
 C_AFTER = 14
 
-V_RG = 0.000428
-S_RG = 0.000836
-T_Q = 0.91
-COST = {"acopy": 0.49, "aquant": 0.46, "gate": 1.1, "mix": 0.91, "tanh_c": 0.91,
-        "ctrans": 0.0, "ccopy": 0.49, "sum_c": 0.0}
+BASE_SPLIT = 512
+SPLIT_SHIFT = {"act_copy": 96, "act_quantise": -88, "gate_act": 216, "gate_mix": -176, "tanh_c": 176,
+               "c_transpose": 0, "c_copy": 96}
+NO_QUANTISE_SHIFT = 184
 
 
 def bank_of(gi, j):
@@ -47,38 +47,33 @@ def tile_vlstmcell_kernel(tc, inputs, h_tm1, c_tm1, z_tm1, kernel, recurrent_ker
         rawp = ctx.enter_context(tc.tile_pool(name="rawp", bufs=RAW_BUFS))
         grpp = ctx.enter_context(tc.tile_pool(name="grpp", bufs=GRP_BUFS))
         codp = ctx.enter_context(tc.tile_pool(name="codp", bufs=COD_BUFS))
-        tmpp = ctx.enter_context(tc.tile_pool(name="tmpp", bufs=3))
+        tmpp = ctx.enter_context(tc.tile_pool(name="tmpp", bufs=TMP_BUFS))
         psum = ctx.enter_context(tc.psum_pool(name="psum", bufs=1))
         ctx.enter_context(tc.manual_schedule())
 
-        slots = N_STREAM
-        s_work = [[] for k in range(slots + 8)]
-        v_work = [[] for k in range(slots + 8)]
-        p_work = [[] for k in range(slots + 8)]
-        s_work[0] += [("acopy", 1, 0), ("acopy", 1, 1)]
-        v_work[1] += [("aquant", 1, 0)]
-        s_work[1] += [("acopy", 2, 0), ("acopy", 2, 1)]
-        v_work[2] += [("aquant", 2, 0)]
+        s_work = [[] for k in range(N_STREAM)]
+        v_work = [[] for k in range(N_STREAM)]
+        p_work = [[] for k in range(N_STREAM)]
+        s_work[0] += [("act_copy", 1, 0), ("act_copy", 1, 1)]
+        v_work[1] += [("act_quantise", 1, 0)]
+        s_work[1] += [("act_copy", 2, 0), ("act_copy", 2, 1)]
+        v_work[2] += [("act_quantise", 2, 0)]
         for gi in range(3):
-            e = PASSES * gi + PASSES - 1
+            last = PASSES * gi + PASSES - 1
             for hh in range(2):
-                s_work[e + 2 + hh].append(("gate", gi, hh))
+                first = last + 2 + (hh if gi < 2 else 0)
+                s_work[first].append(("gate_act", gi, hh))
                 if gi >= 1:
-                    v_work[e + 3 + hh].append(("mix", gi, hh))
+                    v_work[first + 1].append(("gate_mix", gi, hh))
                 if gi == 2:
-                    p_work[e + 3 + hh].append(("sum_c", gi, hh))
-                    s_work[e + 4 + hh].append(("tanh_c", gi, hh))
-        s_work[14].append(("ctrans", 0, 0))
-        s_work[15] += [("ccopy", 0, 0), ("ccopy", 0, 1)]
+                    p_work[first + 1].append(("sum_c", gi, hh))
+                    s_work[first + 2].append(("tanh_c", gi, hh))
+        s_work[14].append(("c_transpose", 0, 0))
+        s_work[15] += [("c_copy", 0, 0), ("c_copy", 0, 1)]
 
         def split(s):
-            s_fix = sum(COST[w[0]] for w in s_work[s])
-            v_fix = sum(COST[w[0]] for w in v_work[s]) + (T_Q if s >= 1 else 0.0)
-            cv = (s_fix + 4 * U * S_RG - v_fix) / (4 * (V_RG + S_RG))
-            cv = 8 * int(round(cv / 8))
-            if cv > U - 64:
-                return U
-            return max(cv, 64)
+            shift = sum(SPLIT_SHIFT[w[0]] for w in s_work[s] + v_work[s])
+            return BASE_SPLIT + shift + (NO_QUANTISE_SHIFT if s == 0 else 0)
 
         ident_f = const.tile([P, P], F32)
         make_identity(nc, ident_f[:])
@@ -131,6 +126,7 @@ def tile_vlstmcell_kernel(tc, inputs, h_tm1, c_tm1, z_tm1, kernel, recurrent_ker
         cT = const.tile([P, NJ, B], BF16)
         state = const.tile([P, NJ, B], F32)
         th = const.tile([P, 2, U], F32)
+
         bank_free = [False] * 6 + [True, True]
         a_ready = [False] * 3
         grouped = {}
@@ -163,7 +159,7 @@ def tile_vlstmcell_kernel(tc, inputs, h_tm1, c_tm1, z_tm1, kernel, recurrent_ker
                 nc.scalar.copy(out=dst, in_=srcv)
             bank_free[2 * s + gl] = True
 
-        def act_quant(s):
+        def act_quantise(s):
             nc.vector.quantize_mx(out=a_codes[:, 512 * s:512 * s + 512].bitcast(FP8X4),
                                   scales=a_scales[:, 512 * s:512 * s + 512], in_=ga[s][:])
             a_ready[s] = True
@@ -173,9 +169,8 @@ def tile_vlstmcell_kernel(tc, inputs, h_tm1, c_tm1, z_tm1, kernel, recurrent_ker
             grp = grpp.tile([P, U, 4], BF16, align_bytes=64, name="grp")
             nc.vector.tensor_copy(out=grp[:, 0:cv, :].rearrange("p (c i) t -> p c t i", i=4),
                                   in_=raw[:, :, 0:cv].rearrange("p t (c i) -> p c t i", i=4))
-            if cv < U:
-                nc.scalar.copy(out=grp[:, cv:U, :].rearrange("p (c i) t -> p c t i", i=4),
-                               in_=raw[:, :, cv:U].rearrange("p t (c i) -> p c t i", i=4))
+            nc.scalar.copy(out=grp[:, cv:U, :].rearrange("p (c i) t -> p c t i", i=4),
+                           in_=raw[:, :, cv:U].rearrange("p t (c i) -> p c t i", i=4))
             grouped[i] = grp
 
         def quantise(i):
@@ -192,7 +187,7 @@ def tile_vlstmcell_kernel(tc, inputs, h_tm1, c_tm1, z_tm1, kernel, recurrent_ker
             c = i % PASSES
             return i in coded and a_ready[c // 2] and (c != 0 or bank_free[b])
 
-        def flush_pe():
+        def multiply_what_is_ready():
             while True:
                 cand = [pe_queue[b][pe_head[b]] + (b,) for b in range(NJ) if ready(b)]
                 if not cand:
@@ -225,7 +220,7 @@ def tile_vlstmcell_kernel(tc, inputs, h_tm1, c_tm1, z_tm1, kernel, recurrent_ker
                                          bias=hb[:, 8 * g + j:8 * g + j + 1], scale=0.2)
                 bank_free[j] = not (gi == 2 and hh == 0)
 
-        def mix(gi, hh):
+        def gate_mix(gi, hh):
             js = slice(4 * hh, 4 * hh + 4)
             tmp = tmp_of[(gi, hh)]
             if gi == 2:
@@ -251,38 +246,44 @@ def tile_vlstmcell_kernel(tc, inputs, h_tm1, c_tm1, z_tm1, kernel, recurrent_ker
                 nc.scalar.activation(out=th[:, m, 512 * hh:512 * hh + 512], in_=ct[(hh, m)][:], func=ACT.Tanh)
                 bank_free[2 * hh + m] = True
 
+        def c_transpose():
+            for hh in range(2):
+                c_ps[hh] = psum.tile([P, 4, B], BF16, tag="b%d" % (6 + hh), name="c_ps")
+                bank_free[6 + hh] = False
+                for jj in range(4):
+                    for m in range(2):
+                        col = U * m + P * (4 * hh + jj)
+                        nc.tensor.transpose(c_ps[hh][:, jj, P * m:P * m + P], c_sb[0][:, col:col + P], ident_b[:])
+
+        def c_copy(hh):
+            nc.scalar.copy(out=cT[:, 4 * hh:4 * hh + 4, :], in_=c_ps[hh][:])
+            bank_free[6 + hh] = True
+
         def do(w):
             kind, a, b = w
-            if kind == "acopy":
+            if kind == "act_copy":
                 act_copy(a, b, "s")
-            elif kind == "aquant":
-                act_quant(a)
-            elif kind == "gate":
+            elif kind == "act_quantise":
+                act_quantise(a)
+            elif kind == "gate_act":
                 gate_act(a, b)
-            elif kind == "mix":
-                mix(a, b)
+            elif kind == "gate_mix":
+                gate_mix(a, b)
             elif kind == "sum_c":
                 sum_c(b)
             elif kind == "tanh_c":
                 tanh_c(b)
-            elif kind == "ctrans":
-                for hh in range(2):
-                    c_ps[hh] = psum.tile([P, 4, B], BF16, tag="b%d" % (6 + hh), name="c_ps")
-                    bank_free[6 + hh] = False
-                    for jj in range(4):
-                        for m in range(2):
-                            col = U * m + P * (4 * hh + jj)
-                            nc.tensor.transpose(c_ps[hh][:, jj, P * m:P * m + P], c_sb[0][:, col:col + P], ident_b[:])
-            elif kind == "ccopy":
-                nc.scalar.copy(out=cT[:, 4 * b:4 * b + 4, :], in_=c_ps[b][:])
-                bank_free[6 + b] = True
+            elif kind == "c_transpose":
+                c_transpose()
+            elif kind == "c_copy":
+                c_copy(b)
 
         act_copy(0, 0, "v")
         act_copy(0, 1, "s")
-        act_quant(0)
+        act_quantise(0)
 
         next_load = [RAW_BUFS]
-        for s in range(slots):
+        for s in range(N_STREAM):
             regroup(s, split(s))
             if next_load[0] < N_UNITS:
                 load_unit(next_load[0])
@@ -295,7 +296,7 @@ def tile_vlstmcell_kernel(tc, inputs, h_tm1, c_tm1, z_tm1, kernel, recurrent_ker
                 do(w)
             for w in v_work[s]:
                 do(w)
-            flush_pe()
+            multiply_what_is_ready()
             for w in p_work[s]:
                 do(w)
 
@@ -346,24 +347,15 @@ def tile_vlstmcell_kernel(tc, inputs, h_tm1, c_tm1, z_tm1, kernel, recurrent_ker
                                            op0=ALU.min, op1=ALU.mult)
             nc.sync.dma_start(out=out_v[:, :, BW * q:BW * q + BW], in_=dst)
 
-        block_regroup(0)
-        quantise(N_STREAM - 1)
-        flush_pe()
-        block_regroup(1)
-        block_multiply(0)
-        for w in s_work[N_STREAM]:
-            do(w)
-        flush_pe()
-        block_regroup(2)
-        block_multiply(1)
-        block_act(0)
-        block_regroup(3)
-        block_multiply(2)
-        block_act(1)
-        block_finish(0)
-        block_multiply(3)
-        block_act(2)
-        block_finish(1)
-        block_act(3)
-        block_finish(2)
-        block_finish(3)
+        for step in range(7):
+            if step < 4:
+                block_regroup(step)
+            if step == 0:
+                quantise(N_STREAM - 1)
+                multiply_what_is_ready()
+            if 1 <= step < 5:
+                block_multiply(step - 1)
+            if 2 <= step < 6:
+                block_act(step - 2)
+            if step >= 3:
+                block_finish(step - 3)

@@ -28,7 +28,7 @@ COD_BUFS = 8
 TMP_BUFS = 3
 C_AFTER = 14
 
-BASE_SPLIT = 512
+BASE_SPLIT = 480
 SPLIT_SHIFT = {"act_copy": 96, "act_quantise": -88, "gate_act": 216, "gate_mix": -176, "tanh_c": 176,
                "c_transpose": 0, "c_copy": 96}
 NO_QUANTISE_SHIFT = 184

@@ -29,6 +29,7 @@ TMP_BUFS = 3
 C_AFTER = 14
 
 BASE_SPLIT = 480
+RUN = 8
 SPLIT_SHIFT = {"act_copy": 96, "act_quantise": -88, "gate_act": 216, "gate_mix": -176, "tanh_c": 176,
                "c_transpose": 0, "c_copy": 96}
 NO_QUANTISE_SHIFT = 184
@@ -73,7 +74,8 @@ def tile_vlstmcell_kernel(tc, inputs, h_tm1, c_tm1, z_tm1, kernel, recurrent_ker
 
         def split(s):
             shift = sum(SPLIT_SHIFT[w[0]] for w in s_work[s] + v_work[s])
-            return BASE_SPLIT + shift + (NO_QUANTISE_SHIFT if s == 0 else 0)
+            cv = BASE_SPLIT + shift + (NO_QUANTISE_SHIFT if s == 0 else 0)
+            return cv - cv % (2 * RUN)
 
         ident_f = const.tile([P, P], F32)
         make_identity(nc, ident_f[:])
@@ -167,10 +169,10 @@ def tile_vlstmcell_kernel(tc, inputs, h_tm1, c_tm1, z_tm1, kernel, recurrent_ker
         def regroup(i, cv):
             raw = raws[i]
             grp = grpp.tile([P, U, 4], BF16, align_bytes=64, name="grp")
-            nc.vector.tensor_copy(out=grp[:, 0:cv, :].rearrange("p (c i) t -> p c t i", i=4),
-                                  in_=raw[:, :, 0:cv].rearrange("p t (c i) -> p c t i", i=4))
-            nc.scalar.copy(out=grp[:, cv:U, :].rearrange("p (c i) t -> p c t i", i=4),
-                           in_=raw[:, :, cv:U].rearrange("p t (c i) -> p c t i", i=4))
+            nc.vector.tensor_copy(out=grp[:, 0:cv, :].rearrange("p (c i) t -> p c t i", i=RUN),
+                                  in_=raw[:, :, 0:cv].rearrange("p t (c i) -> p c t i", i=RUN))
+            nc.scalar.copy(out=grp[:, cv:U, :].rearrange("p (c i) t -> p c t i", i=RUN),
+                           in_=raw[:, :, cv:U].rearrange("p t (c i) -> p c t i", i=RUN))
             grouped[i] = grp
 
         def quantise(i):
@@ -307,10 +309,10 @@ def tile_vlstmcell_kernel(tc, inputs, h_tm1, c_tm1, z_tm1, kernel, recurrent_ker
         def block_regroup(q):
             grp = grpp.tile([P, U, 4], BF16, align_bytes=64, name="grp")
             cols = slice(BW * q, BW * q + BW)
-            nc.vector.tensor_copy(out=grp[:, 0:BW, :].rearrange("p (c i) t -> p c t i", i=4),
-                                  in_=raws[N_STREAM][:, :, cols].rearrange("p t (c i) -> p c t i", i=4))
-            nc.scalar.copy(out=grp[:, BW:2 * BW, :].rearrange("p (c i) t -> p c t i", i=4),
-                           in_=raws[N_STREAM + 1][:, :, cols].rearrange("p t (c i) -> p c t i", i=4))
+            nc.vector.tensor_copy(out=grp[:, 0:BW, :].rearrange("p (c i) t -> p c t i", i=RUN),
+                                  in_=raws[N_STREAM][:, :, cols].rearrange("p t (c i) -> p c t i", i=RUN))
+            nc.scalar.copy(out=grp[:, BW:2 * BW, :].rearrange("p (c i) t -> p c t i", i=RUN),
+                           in_=raws[N_STREAM + 1][:, :, cols].rearrange("p t (c i) -> p c t i", i=RUN))
             blk[q] = grp
 
         def block_multiply(q):

@@ -21,7 +21,7 @@ PASSES = 6
 GATE_ORDER = (2, 0, 1, 3)
 N_UNITS = 4 * PASSES
 N_STREAM = N_UNITS - 2
-BW = 256
+BLOCKS = ((0, 2), (2, 2), (4, 2), (6, 1), (7, 1))
 RAW_BUFS = 8
 GRP_BUFS = 3
 COD_BUFS = 8
@@ -55,10 +55,10 @@ def tile_vlstmcell_kernel(tc, inputs, h_tm1, c_tm1, z_tm1, kernel, recurrent_ker
         s_work = [[] for k in range(N_STREAM)]
         v_work = [[] for k in range(N_STREAM)]
         p_work = [[] for k in range(N_STREAM)]
-        s_work[0] += [("act_copy", 1, 0), ("act_copy", 1, 1)]
-        v_work[1] += [("act_quantise", 1, 0)]
-        s_work[1] += [("act_copy", 2, 0), ("act_copy", 2, 1)]
-        v_work[2] += [("act_quantise", 2, 0)]
+        s_work[1] += [("act_copy", 1, 0), ("act_copy", 1, 1)]
+        v_work[2] += [("act_quantise", 1, 0)]
+        s_work[3] += [("act_copy", 2, 0), ("act_copy", 2, 1)]
+        v_work[4] += [("act_quantise", 2, 0)]
         for gi in range(3):
             last = PASSES * gi + PASSES - 1
             for hh in range(2):
@@ -107,10 +107,12 @@ def tile_vlstmcell_kernel(tc, inputs, h_tm1, c_tm1, z_tm1, kernel, recurrent_ker
 
         x_sb = load_act(inputs, "x_sb")
         load_unit(0)
-        h_sb = load_act(h_tm1, "h_sb")
         load_unit(1)
+        h_sb = load_act(h_tm1, "h_sb")
+        load_unit(2)
+        load_unit(3)
         z_sb = load_act(z_tm1, "z_sb")
-        for i in range(2, RAW_BUFS):
+        for i in range(4, RAW_BUFS):
             load_unit(i)
         acts = (x_sb, h_sb, z_sb)
         c_sb = {}
@@ -308,23 +310,27 @@ def tile_vlstmcell_kernel(tc, inputs, h_tm1, c_tm1, z_tm1, kernel, recurrent_ker
 
         def block_regroup(q):
             grp = grpp.tile([P, U, 4], BF16, align_bytes=64, name="grp")
-            cols = slice(BW * q, BW * q + BW)
-            nc.vector.tensor_copy(out=grp[:, 0:BW, :].rearrange("p (c i) t -> p c t i", i=RUN),
+            j0, nj = BLOCKS[q]
+            bw = P * nj
+            cols = slice(P * j0, P * j0 + bw)
+            nc.vector.tensor_copy(out=grp[:, 0:bw, :].rearrange("p (c i) t -> p c t i", i=RUN),
                                   in_=raws[N_STREAM][:, :, cols].rearrange("p t (c i) -> p c t i", i=RUN))
-            nc.scalar.copy(out=grp[:, BW:2 * BW, :].rearrange("p (c i) t -> p c t i", i=RUN),
+            nc.scalar.copy(out=grp[:, bw:2 * bw, :].rearrange("p (c i) t -> p c t i", i=RUN),
                            in_=raws[N_STREAM + 1][:, :, cols].rearrange("p t (c i) -> p c t i", i=RUN))
             blk[q] = grp
 
         def block_multiply(q):
             codes = codp.tile([P, U], U32, align_bytes=64, name="codes")
             scales = codp.tile([P, U], U8, align_bytes=64, name="scales")
-            nc.vector.quantize_mx(out=codes[:, 0:2 * BW].bitcast(FP8X4), scales=scales[:, 0:2 * BW],
-                                  in_=blk[q][:, 0:2 * BW, :].rearrange("p w j -> p (w j)"))
+            j0, nj = BLOCKS[q]
+            bw = P * nj
+            nc.vector.quantize_mx(out=codes[:, 0:2 * bw].bitcast(FP8X4), scales=scales[:, 0:2 * bw],
+                                  in_=blk[q][:, 0:2 * bw, :].rearrange("p w j -> p (w j)"))
             for cc in range(2):
                 c = PASSES - 2 + cc
-                for jj in range(2):
-                    w0 = BW * cc + P * jj
-                    nc.tensor.matmul_mx(out=acc[(3, 2 * q + jj)][:],
+                for jj in range(nj):
+                    w0 = bw * cc + P * jj
+                    nc.tensor.matmul_mx(out=acc[(3, j0 + jj)][:],
                                         lhsT=codes[:, w0:w0 + P].bitcast(FP8X4),
                                         lhsT_scale=scales[:, w0:w0 + P],
                                         rhs=a_codes[:, B * c:B * c + B].bitcast(FP8X4),
@@ -334,30 +340,33 @@ def tile_vlstmcell_kernel(tc, inputs, h_tm1, c_tm1, z_tm1, kernel, recurrent_ker
         def block_act(q):
             g = GATE_ORDER[3]
             tmp = tmpp.tile([P, 4, B], F32, name="tmp")
-            for jj in range(2):
-                j = 2 * q + jj
+            j0, nj = BLOCKS[q]
+            for jj in range(nj):
+                j = j0 + jj
                 nc.scalar.activation(out=tmp[:, jj, :], in_=acc[(3, j)][:], func=ACT.Relu,
                                      bias=hb[:, 8 * g + j:8 * g + j + 1], scale=0.2)
-            hp[q] = psum.tile([P, 2, BW], F32, tag="b%d" % bank_of(3, 2 * q), name="hp")
+            hp[q] = psum.tile([P, 2, P * nj], F32, tag="b%d" % bank_of(3, j0), name="hp")
             for m in range(2):
-                for jj in range(2):
+                for jj in range(nj):
                     nc.tensor.transpose(hp[q][:, m, P * jj:P * jj + P], tmp[:, jj, P * m:P * m + P], ident_f[:])
 
         def block_finish(q):
-            dst = th[:, :, BW * q:BW * q + BW]
+            j0, nj = BLOCKS[q]
+            dst = th[:, :, P * j0:P * (j0 + nj)]
             nc.vector.scalar_tensor_tensor(out=dst, in0=hp[q][:], scalar=1.0, in1=dst,
                                            op0=ALU.min, op1=ALU.mult)
-            nc.sync.dma_start(out=out_v[:, :, BW * q:BW * q + BW], in_=dst)
+            nc.sync.dma_start(out=out_v[:, :, P * j0:P * (j0 + nj)], in_=dst)
 
-        for step in range(7):
-            if step < 4:
+        nb = len(BLOCKS)
+        for step in range(nb + 3):
+            if step < nb:
                 block_regroup(step)
             if step == 0:
                 quantise(N_STREAM - 1)
                 multiply_what_is_ready()
-            if 1 <= step < 5:
+            if 1 <= step < nb + 1:
                 block_multiply(step - 1)
-            if 2 <= step < 6:
+            if 2 <= step < nb + 2:
                 block_act(step - 2)
             if step >= 3:
                 block_finish(step - 3)

@@ -31,7 +31,7 @@ C_AFTER = 14
 BASE_SPLIT = 480
 RUN = 8
 SPLIT_SHIFT = {"act_copy": 96, "act_quantise": -88, "gate_act": 216, "gate_mix": -176, "tanh_c": 176,
-               "c_transpose": 0, "c_copy": 96}
+               "c_transpose": 0}
 NO_QUANTISE_SHIFT = 184
 
 
@@ -63,14 +63,14 @@ def tile_vlstmcell_kernel(tc, inputs, h_tm1, c_tm1, z_tm1, kernel, recurrent_ker
             last = PASSES * gi + PASSES - 1
             for hh in range(2):
                 first = last + 2 + (hh if gi < 2 else 0)
+                if gi == 2 and hh == 1:
+                    s_work[first].append(("c_transpose", 0, 0))
                 s_work[first].append(("gate_act", gi, hh))
                 if gi >= 1:
                     v_work[first + 1].append(("gate_mix", gi, hh))
                 if gi == 2:
                     p_work[first + 1].append(("sum_c", gi, hh))
                     s_work[first + 2].append(("tanh_c", gi, hh))
-        s_work[14].append(("c_transpose", 0, 0))
-        s_work[15] += [("c_copy", 0, 0), ("c_copy", 0, 1)]
 
         def split(s):
             shift = sum(SPLIT_SHIFT[w[0]] for w in s_work[s] + v_work[s])
@@ -127,7 +127,6 @@ def tile_vlstmcell_kernel(tc, inputs, h_tm1, c_tm1, z_tm1, kernel, recurrent_ker
         a_codes = const.tile([P, PASSES * B], U32, align_bytes=64)
         a_scales = const.tile([P, PASSES * B], U8, align_bytes=64)
         ga = [const.tile([P, 2 * 4 * B], BF16, align_bytes=64, name="ga%d" % s) for s in range(3)]
-        cT = const.tile([P, NJ, B], BF16)
         state = const.tile([P, NJ, B], F32)
         th = const.tile([P, 2, U], F32)
 
@@ -229,7 +228,7 @@ def tile_vlstmcell_kernel(tc, inputs, h_tm1, c_tm1, z_tm1, kernel, recurrent_ker
             tmp = tmp_of[(gi, hh)]
             if gi == 2:
                 nc.vector.scalar_tensor_tensor(out=flat(tmp[:]), in0=flat(tmp[:]), scalar=1.0,
-                                               in1=flat(cT[:, js, :]), op0=ALU.min, op1=ALU.mult)
+                                               in1=flat(c_ps[hh][:]), op0=ALU.min, op1=ALU.mult)
             else:
                 st = flat(state[:, js, :])
                 nc.vector.scalar_tensor_tensor(out=st, in0=flat(tmp[:]), scalar=1.0, in1=st,
@@ -252,16 +251,11 @@ def tile_vlstmcell_kernel(tc, inputs, h_tm1, c_tm1, z_tm1, kernel, recurrent_ker
 
         def c_transpose():
             for hh in range(2):
-                c_ps[hh] = psum.tile([P, 4, B], BF16, tag="b%d" % (6 + hh), name="c_ps")
-                bank_free[6 + hh] = False
+                c_ps[hh] = psum.tile([P, 4, B], BF16, tag="b%d" % (2 + hh), name="c_ps")
                 for jj in range(4):
                     for m in range(2):
                         col = U * m + P * (4 * hh + jj)
                         nc.tensor.transpose(c_ps[hh][:, jj, P * m:P * m + P], c_sb[0][:, col:col + P], ident_b[:])
-
-        def c_copy(hh):
-            nc.scalar.copy(out=cT[:, 4 * hh:4 * hh + 4, :], in_=c_ps[hh][:])
-            bank_free[6 + hh] = True
 
         def do(w):
             kind, a, b = w
@@ -279,8 +273,6 @@ def tile_vlstmcell_kernel(tc, inputs, h_tm1, c_tm1, z_tm1, kernel, recurrent_ker
                 tanh_c(b)
             elif kind == "c_transpose":
                 c_transpose()
-            elif kind == "c_copy":
-                c_copy(b)
 
         act_copy(0, 0, "v")
         act_copy(0, 1, "s")

@@ -22,8 +22,8 @@ GATE_ORDER = (2, 0, 1, 3)
 N_UNITS = 4 * PASSES
 N_STREAM = N_UNITS - 2
 BLOCKS = ((0, 2), (2, 2), (4, 2), (6, 1), (7, 1))
-RAW_BUFS = 8
-GRP_BUFS = 3
+RAW_BUFS = 10
+GRP_BUFS = 5
 COD_BUFS = 8
 TMP_BUFS = 3
 C_AFTER = 14

@@ -26,11 +26,11 @@ RAW_BUFS = 10
 GRP_BUFS = 5
 COD_BUFS = 8
 TMP_BUFS = 3
-C_AFTER = 14
+C_AFTER = 19
 
 BASE_SPLIT = 480
 RUN = 8
-SPLIT_SHIFT = {"act_copy": 96, "act_quantise": -88, "gate_act": 216, "gate_mix": -176, "tanh_c": 176,
+SPLIT_SHIFT = {"act_copy": 96, "act_quantise": -88, "gate_act": 216, "gate_mix": -176, "tanh_c": 216,
                "c_transpose": 0}
 NO_QUANTISE_SHIFT = 184
 

@@ -21,8 +21,8 @@ PASSES = 6
 GATE_ORDER = (2, 0, 1, 3)
 N_UNITS = 4 * PASSES
 N_STREAM = N_UNITS - 2
-BLOCKS = ((0, 2), (2, 2), (4, 2), (6, 1), (7, 1))
-RAW_BUFS = 10
+BLOCKS = ((0, 2), (2, 2), (4, 2), (6, 2))
+RAW_BUFS = 9
 GRP_BUFS = 5
 COD_BUFS = 8
 TMP_BUFS = 3
@@ -30,13 +30,15 @@ C_AFTER = 19
 
 BASE_SPLIT = 480
 RUN = 8
-SPLIT_SHIFT = {"act_copy": 96, "act_quantise": -88, "gate_act": 216, "gate_mix": -176, "tanh_c": 216,
-               "c_transpose": 0}
+SPLIT_SHIFT = {"act_copy": 96, "act_quantise": -88, "gate_act": 216, "gate_mix": -176, "tanh_c": 176,
+               "c_transpose": 0, "pe_regroup": -64}
+PE_COLS = 256
+PE_UNITS = (4, 5, 9, 10, 11, 15, 16, 17)
 NO_QUANTISE_SHIFT = 184
 
 
 def bank_of(gi, j):
-    return j if gi < 3 else (j + 4) % NJ
+    return 4 * (gi % 2) + j // 2
 
 
 def tile_vlstmcell_kernel(tc, inputs, h_tm1, c_tm1, z_tm1, kernel, recurrent_kernel,
@@ -73,7 +75,7 @@ def tile_vlstmcell_kernel(tc, inputs, h_tm1, c_tm1, z_tm1, kernel, recurrent_ker
                     s_work[first + 2].append(("tanh_c", gi, hh))
 
         def split(s):
-            shift = sum(SPLIT_SHIFT[w[0]] for w in s_work[s] + v_work[s])
+            shift = sum(SPLIT_SHIFT[w[0]] for w in s_work[s] + v_work[s]) + (SPLIT_SHIFT["pe_regroup"] if s in PE_UNITS else 0)
             cv = BASE_SPLIT + shift + (NO_QUANTISE_SHIFT if s == 0 else 0)
             return cv - cv % (2 * RUN)
 
@@ -124,32 +126,39 @@ def tile_vlstmcell_kernel(tc, inputs, h_tm1, c_tm1, z_tm1, kernel, recurrent_ker
         hb = const.tile([P, 32], F32)
         nc.vector.tensor_scalar(out=hb[:], in0=b32[:], scalar1=0.2, scalar2=0.5, op0=ALU.mult, op1=ALU.add)
 
-        a_codes = const.tile([P, PASSES * B], U32, align_bytes=64)
-        a_scales = const.tile([P, PASSES * B], U8, align_bytes=64)
+        a_codes = const.tile([P, B + PASSES * B], U32, align_bytes=64)
+        a_scales = const.tile([P, B + PASSES * B], U8, align_bytes=64)
+        nc.vector.memset(a_codes[:, 0:B], 0)
+        nc.vector.memset(a_scales[:, 0:B].bitcast(U32), 0)
         ga = [const.tile([P, 2 * 4 * B], BF16, align_bytes=64, name="ga%d" % s) for s in range(3)]
         state = const.tile([P, NJ, B], F32)
         th = const.tile([P, 2, U], F32)
 
-        bank_free = [False] * 6 + [True, True]
+        bank_free = [True] * 4 + [False] * 4
         a_ready = [False] * 3
         grouped = {}
         coded = {}
         acc = {}
         tmp_of = {}
         c_ps = {}
+        reg_of = {}
         ct = {}
         pe_queue = [[] for b in range(NJ)]
-        for i in range(N_STREAM):
+        for i in range(N_UNITS):
+            c = i % PASSES
             for j in range(NJ):
-                pe_queue[bank_of(i // PASSES, j)].append((i, j))
+                pe_queue[bank_of(i // PASSES, j)].append((i, j ^ 1 if c == 0 else j))
         pe_head = [0] * NJ
+
+        def half(j):
+            return slice(B * (j % 2), B * (j % 2) + B)
 
         def flat(ap):
             return ap.rearrange("p j b -> p (j b)")
 
         def act_copy(s, gl, eng):
             a32 = acts[s][:].bitcast(F32)
-            xt = psum.tile([P, 2, B], F32, tag="b%d" % (2 * s + gl), name="xt")
+            xt = psum.tile([P, 2, B], F32, tag="b%d" % (4 + (2 * s + gl) % 4), name="xt")
             for m in range(2):
                 for u in range(2):
                     w0 = 512 * m + 256 * gl
@@ -160,11 +169,11 @@ def tile_vlstmcell_kernel(tc, inputs, h_tm1, c_tm1, z_tm1, kernel, recurrent_ker
                 nc.vector.tensor_copy(out=dst, in_=srcv)
             else:
                 nc.scalar.copy(out=dst, in_=srcv)
-            bank_free[2 * s + gl] = True
+            bank_free[4 + (2 * s + gl) % 4] = s > 0
 
         def act_quantise(s):
-            nc.vector.quantize_mx(out=a_codes[:, 512 * s:512 * s + 512].bitcast(FP8X4),
-                                  scales=a_scales[:, 512 * s:512 * s + 512], in_=ga[s][:])
+            cols = slice(B + 512 * s, B + 512 * s + 512)
+            nc.vector.quantize_mx(out=a_codes[:, cols].bitcast(FP8X4), scales=a_scales[:, cols], in_=ga[s][:])
             a_ready[s] = True
 
         def regroup(i, cv):
@@ -172,23 +181,40 @@ def tile_vlstmcell_kernel(tc, inputs, h_tm1, c_tm1, z_tm1, kernel, recurrent_ker
             grp = grpp.tile([P, U, 4], BF16, align_bytes=64, name="grp")
             nc.vector.tensor_copy(out=grp[:, 0:cv, :].rearrange("p (c i) t -> p c t i", i=RUN),
                                   in_=raw[:, :, 0:cv].rearrange("p t (c i) -> p c t i", i=RUN))
-            nc.scalar.copy(out=grp[:, cv:U, :].rearrange("p (c i) t -> p c t i", i=RUN),
-                           in_=raw[:, :, cv:U].rearrange("p t (c i) -> p c t i", i=RUN))
+            end = U - PE_COLS if i in PE_UNITS else U
+            nc.scalar.copy(out=grp[:, cv:end, :].rearrange("p (c i) t -> p c t i", i=RUN),
+                           in_=raw[:, :, cv:end].rearrange("p t (c i) -> p c t i", i=RUN))
+            if i in PE_UNITS:
+                nc.scalar.copy(out=grp[:, end:U, :].rearrange("p c t -> p (c t)"), in_=reg_of[i][:].rearrange("p c t -> p (c t)"))
+                if i + 1 not in PE_UNITS:
+                    bank_free[reg_bank(i)] = True
             grouped[i] = grp
+
+        def reg_bank(i):
+            return 7 if i // PASSES % 2 == 0 else 3
+
+        def pe_regroup(i):
+            bank_free[reg_bank(i)] = False
+            reg = psum.tile([P, PE_COLS, 4], BF16, tag="b%d" % reg_bank(i), name="reg")
+            for h in range(2):
+                nc.tensor.matmul(reg[:, :, 2 * h:2 * h + 2].rearrange("p c t -> p t c"), lhsT=ident_b[:],
+                                 rhs=raws[i][:, 2 * h:2 * h + 2, U - PE_COLS:U], start=True, stop=True)
+            reg_of[i] = reg
 
         def quantise(i):
             codes = codp.tile([P, U], U32, align_bytes=64, name="codes")
             scales = codp.tile([P, U], U8, align_bytes=64, name="scales")
             nc.vector.quantize_mx(out=codes[:].bitcast(FP8X4), scales=scales[:],
                                   in_=grouped[i][:].rearrange("p w j -> p (w j)"))
-            coded[i] = (codes, scales)
+            for j in range(NJ):
+                coded[(i, j)] = (codes, scales, P * j)
 
         def ready(b):
             if pe_head[b] >= len(pe_queue[b]):
                 return False
             i, j = pe_queue[b][pe_head[b]]
             c = i % PASSES
-            return i in coded and a_ready[c // 2] and (c != 0 or bank_free[b])
+            return (i, j) in coded and a_ready[c // 2] and (c != 0 or bank_free[b] or j % 2 == 0)
 
         def multiply_what_is_ready():
             while True:
@@ -197,16 +223,17 @@ def tile_vlstmcell_kernel(tc, inputs, h_tm1, c_tm1, z_tm1, kernel, recurrent_ker
                     return
                 i, j, b = min(cand)
                 gi, c = divmod(i, PASSES)
-                if c == 0:
-                    acc[(gi, j)] = psum.tile([P, B], F32, tag="b%d" % b, name="acc")
+                opens, closes = c == 0 and j % 2 == 1, c == PASSES - 1 and j % 2 == 1
+                if opens:
+                    acc[(gi, j // 2)] = psum.tile([P, 2 * B], F32, tag="b%d" % b, name="acc")
                     bank_free[b] = False
-                codes, scales = coded[i]
-                nc.tensor.matmul_mx(out=acc[(gi, j)][:],
-                                    lhsT=codes[:, P * j:P * j + P].bitcast(FP8X4),
-                                    lhsT_scale=scales[:, P * j:P * j + P],
-                                    rhs=a_codes[:, B * c:B * c + B].bitcast(FP8X4),
-                                    rhs_scale=a_scales[:, B * c:B * c + B],
-                                    start=(c == 0), stop=(c == PASSES - 1))
+                codes, scales, w0 = coded[(i, j)]
+                moving = slice(0, 2 * B) if opens else slice(B + B * c, 2 * B + B * c)
+                place = slice(0, 2 * B) if opens else half(j)
+                nc.tensor.matmul_mx(out=acc[(gi, j // 2)][:, place],
+                                    lhsT=codes[:, w0:w0 + P].bitcast(FP8X4), lhsT_scale=scales[:, w0:w0 + P],
+                                    rhs=a_codes[:, moving].bitcast(FP8X4), rhs_scale=a_scales[:, moving],
+                                    start=opens, stop=closes)
                 pe_head[b] += 1
 
         def gate_act(gi, hh):
@@ -216,12 +243,12 @@ def tile_vlstmcell_kernel(tc, inputs, h_tm1, c_tm1, z_tm1, kernel, recurrent_ker
             for jj in range(4):
                 j = 4 * hh + jj
                 if gi == 0:
-                    nc.scalar.activation(out=state[:, j, :], in_=acc[(gi, j)][:], func=ACT.Tanh,
+                    nc.scalar.activation(out=state[:, j, :], in_=acc[(gi, j // 2)][:, half(j)], func=ACT.Tanh,
                                          bias=b32[:, 8 * g + j:8 * g + j + 1], scale=1.0)
                 else:
-                    nc.scalar.activation(out=tmp_of[(gi, hh)][:, jj, :], in_=acc[(gi, j)][:], func=ACT.Relu,
+                    nc.scalar.activation(out=tmp_of[(gi, hh)][:, jj, :], in_=acc[(gi, j // 2)][:, half(j)], func=ACT.Relu,
                                          bias=hb[:, 8 * g + j:8 * g + j + 1], scale=0.2)
-                bank_free[j] = not (gi == 2 and hh == 0)
+                bank_free[bank_of(gi, j)] = gi < 2
 
         def gate_mix(gi, hh):
             js = slice(4 * hh, 4 * hh + 4)
@@ -236,7 +263,7 @@ def tile_vlstmcell_kernel(tc, inputs, h_tm1, c_tm1, z_tm1, kernel, recurrent_ker
 
         def sum_c(hh):
             for m in range(2):
-                ct[(hh, m)] = psum.tile([P, 512], F32, tag="b%d" % (2 * hh + m), name="ct")
+                ct[(hh, m)] = psum.tile([P, 512], F32, tag="b%d" % (2 - 2 * hh + m), name="ct")
                 for jj in range(4):
                     dst = ct[(hh, m)][:, P * jj:P * jj + P]
                     nc.tensor.matmul(dst, lhsT=state[:, 4 * hh + jj, P * m:P * m + P], rhs=ident_f[:],
@@ -247,11 +274,10 @@ def tile_vlstmcell_kernel(tc, inputs, h_tm1, c_tm1, z_tm1, kernel, recurrent_ker
         def tanh_c(hh):
             for m in range(2):
                 nc.scalar.activation(out=th[:, m, 512 * hh:512 * hh + 512], in_=ct[(hh, m)][:], func=ACT.Tanh)
-                bank_free[2 * hh + m] = True
 
         def c_transpose():
             for hh in range(2):
-                c_ps[hh] = psum.tile([P, 4, B], BF16, tag="b%d" % (2 + hh), name="c_ps")
+                c_ps[hh] = psum.tile([P, 4, B], BF16, tag="b%d" % hh, name="c_ps")
                 for jj in range(4):
                     for m in range(2):
                         col = U * m + P * (4 * hh + jj)
@@ -292,6 +318,8 @@ def tile_vlstmcell_kernel(tc, inputs, h_tm1, c_tm1, z_tm1, kernel, recurrent_ker
                 do(w)
             for w in v_work[s]:
                 do(w)
+            if s + 1 in PE_UNITS:
+                pe_regroup(s + 1)
             multiply_what_is_ready()
             for w in p_work[s]:
                 do(w)
@@ -319,15 +347,9 @@ def tile_vlstmcell_kernel(tc, inputs, h_tm1, c_tm1, z_tm1, kernel, recurrent_ker
             nc.vector.quantize_mx(out=codes[:, 0:2 * bw].bitcast(FP8X4), scales=scales[:, 0:2 * bw],
                                   in_=blk[q][:, 0:2 * bw, :].rearrange("p w j -> p (w j)"))
             for cc in range(2):
-                c = PASSES - 2 + cc
                 for jj in range(nj):
-                    w0 = bw * cc + P * jj
-                    nc.tensor.matmul_mx(out=acc[(3, j0 + jj)][:],
-                                        lhsT=codes[:, w0:w0 + P].bitcast(FP8X4),
-                                        lhsT_scale=scales[:, w0:w0 + P],
-                                        rhs=a_codes[:, B * c:B * c + B].bitcast(FP8X4),
-                                        rhs_scale=a_scales[:, B * c:B * c + B],
-                                        start=False, stop=(cc == 1))
+                    coded[(N_STREAM + cc, j0 + jj)] = (codes, scales, bw * cc + P * jj)
+            multiply_what_is_ready()
 
         def block_act(q):
             g = GATE_ORDER[3]
@@ -335,7 +357,7 @@ def tile_vlstmcell_kernel(tc, inputs, h_tm1, c_tm1, z_tm1, kernel, recurrent_ker
             j0, nj = BLOCKS[q]
             for jj in range(nj):
                 j = j0 + jj
-                nc.scalar.activation(out=tmp[:, jj, :], in_=acc[(3, j)][:], func=ACT.Relu,
+                nc.scalar.activation(out=tmp[:, jj, :], in_=acc[(3, j // 2)][:, half(j)], func=ACT.Relu,
                                      bias=hb[:, 8 * g + j:8 * g + j + 1], scale=0.2)
             hp[q] = psum.tile([P, 2, P * nj], F32, tag="b%d" % bank_of(3, j0), name="hp")
             for m in range(2):

@@ -21,7 +21,7 @@ PASSES = 6
 GATE_ORDER = (2, 0, 1, 3)
 N_UNITS = 4 * PASSES
 N_STREAM = N_UNITS - 2
-BLOCKS = ((0, 2), (2, 2), (4, 2), (6, 2))
+BLOCKS = ((0, 2), (2, 2), (4, 2), (6, 1), (7, 1))
 RAW_BUFS = 9
 GRP_BUFS = 5
 COD_BUFS = 8
@@ -38,7 +38,11 @@ NO_QUANTISE_SHIFT = 184
 
 
 def bank_of(gi, j):
-    return 4 * (gi % 2) + j // 2
+    return 0 if (gi, j) == (3, 7) else 4 * (gi % 2) + j // 2
+
+
+def alone(gi, j):
+    return gi == 3 and j >= 6
 
 
 def tile_vlstmcell_kernel(tc, inputs, h_tm1, c_tm1, z_tm1, kernel, recurrent_kernel,
@@ -147,7 +151,7 @@ def tile_vlstmcell_kernel(tc, inputs, h_tm1, c_tm1, z_tm1, kernel, recurrent_ker
         for i in range(N_UNITS):
             c = i % PASSES
             for j in range(NJ):
-                pe_queue[bank_of(i // PASSES, j)].append((i, j ^ 1 if c == 0 else j))
+                pe_queue[bank_of(i // PASSES, j)].append((i, j ^ 1 if c == 0 and not alone(i // PASSES, j) else j))
         pe_head = [0] * NJ
 
         def half(j):
@@ -214,7 +218,7 @@ def tile_vlstmcell_kernel(tc, inputs, h_tm1, c_tm1, z_tm1, kernel, recurrent_ker
                 return False
             i, j = pe_queue[b][pe_head[b]]
             c = i % PASSES
-            return (i, j) in coded and a_ready[c // 2] and (c != 0 or bank_free[b] or j % 2 == 0)
+            return (i, j) in coded and a_ready[c // 2] and (c != 0 or bank_free[b] or j % 2 == 0 and not alone(i // PASSES, j))
 
         def multiply_what_is_ready():
             while True:
@@ -223,14 +227,16 @@ def tile_vlstmcell_kernel(tc, inputs, h_tm1, c_tm1, z_tm1, kernel, recurrent_ker
                     return
                 i, j, b = min(cand)
                 gi, c = divmod(i, PASSES)
-                opens, closes = c == 0 and j % 2 == 1, c == PASSES - 1 and j % 2 == 1
+                last = j % 2 == 1 or alone(gi, j)
+                opens, closes = c == 0 and last, c == PASSES - 1 and last
                 if opens:
-                    acc[(gi, j // 2)] = psum.tile([P, 2 * B], F32, tag="b%d" % b, name="acc")
+                    acc[b] = psum.tile([P, 2 * B], F32, tag="b%d" % b, name="acc")
                     bank_free[b] = False
                 codes, scales, w0 = coded[(i, j)]
-                moving = slice(0, 2 * B) if opens else slice(B + B * c, 2 * B + B * c)
-                place = slice(0, 2 * B) if opens else half(j)
-                nc.tensor.matmul_mx(out=acc[(gi, j // 2)][:, place],
+                both = opens and not alone(gi, j)
+                moving = slice(0, 2 * B) if both else slice(B + B * c, 2 * B + B * c)
+                place = slice(0, 2 * B) if both else half(j)
+                nc.tensor.matmul_mx(out=acc[b][:, place],
                                     lhsT=codes[:, w0:w0 + P].bitcast(FP8X4), lhsT_scale=scales[:, w0:w0 + P],
                                     rhs=a_codes[:, moving].bitcast(FP8X4), rhs_scale=a_scales[:, moving],
                                     start=opens, stop=closes)
@@ -243,10 +249,10 @@ def tile_vlstmcell_kernel(tc, inputs, h_tm1, c_tm1, z_tm1, kernel, recurrent_ker
             for jj in range(4):
                 j = 4 * hh + jj
                 if gi == 0:
-                    nc.scalar.activation(out=state[:, j, :], in_=acc[(gi, j // 2)][:, half(j)], func=ACT.Tanh,
+                    nc.scalar.activation(out=state[:, j, :], in_=acc[bank_of(gi, j)][:, half(j)], func=ACT.Tanh,
                                          bias=b32[:, 8 * g + j:8 * g + j + 1], scale=1.0)
                 else:
-                    nc.scalar.activation(out=tmp_of[(gi, hh)][:, jj, :], in_=acc[(gi, j // 2)][:, half(j)], func=ACT.Relu,
+                    nc.scalar.activation(out=tmp_of[(gi, hh)][:, jj, :], in_=acc[bank_of(gi, j)][:, half(j)], func=ACT.Relu,
                                          bias=hb[:, 8 * g + j:8 * g + j + 1], scale=0.2)
                 bank_free[bank_of(gi, j)] = gi < 2
 
@@ -274,6 +280,8 @@ def tile_vlstmcell_kernel(tc, inputs, h_tm1, c_tm1, z_tm1, kernel, recurrent_ker
         def tanh_c(hh):
             for m in range(2):
                 nc.scalar.activation(out=th[:, m, 512 * hh:512 * hh + 512], in_=ct[(hh, m)][:], func=ACT.Tanh)
+            if hh == 1:
+                bank_free[0] = True
 
         def c_transpose():
             for hh in range(2):
@@ -357,7 +365,7 @@ def tile_vlstmcell_kernel(tc, inputs, h_tm1, c_tm1, z_tm1, kernel, recurrent_ker
             j0, nj = BLOCKS[q]
             for jj in range(nj):
                 j = j0 + jj
-                nc.scalar.activation(out=tmp[:, jj, :], in_=acc[(3, j // 2)][:, half(j)], func=ACT.Relu,
+                nc.scalar.activation(out=tmp[:, jj, :], in_=acc[bank_of(3, j)][:, half(j)], func=ACT.Relu,
                                      bias=hb[:, 8 * g + j:8 * g + j + 1], scale=0.2)
             hp[q] = psum.tile([P, 2, P * nj], F32, tag="b%d" % bank_of(3, j0), name="hp")
             for m in range(2):

from contextlib import ExitStack

import concourse.mybir as mybir
from concourse.masks import make_identity

FLOPS = 2 * 256 * 3072 * 4096

FP8X4 = mybir.dt.float8_e4m3fn_x4
BF16 = mybir.dt.bfloat16
F32 = mybir.dt.float32
U32 = mybir.dt.uint32
U8 = mybir.dt.uint8
ACT = mybir.ActivationFunctionType
ALU = mybir.AluOpType

P = 128
B = 256
U = 1024
NJ = 8
PASSES = 6
GATE_ORDER = (2, 0, 1, 3)
N_UNITS = 4 * PASSES
N_STREAM = N_UNITS - 2
BLOCKS = ((0, 2), (2, 2), (4, 2), (6, 1), (7, 1))
RAW_BUFS = 9
GRP_BUFS = 5
COD_BUFS = 8
TMP_BUFS = 3
C_AFTER = 19

BASE_SPLIT = 480
RUN = 8
SPLIT_SHIFT = {"act_copy": 96, "act_quantise": -88, "gate_act": 216, "gate_mix": -176, "tanh_c": 176,
               "c_transpose": 0, "pe_regroup": -64}
PE_COLS = 256
PE_UNITS = (4, 5, 9, 10, 11, 15, 16, 17)
NO_QUANTISE_SHIFT = 184


def bank_of(gi, j):
    return 0 if (gi, j) == (3, 7) else 4 * (gi % 2) + j // 2


def alone(gi, j):
    return gi == 3 and j >= 6


def tile_vlstmcell_kernel(tc, inputs, h_tm1, c_tm1, z_tm1, kernel, recurrent_kernel,
                                     recurrent_latent, bias, out):
    nc = tc.nc
    weights = (kernel, recurrent_kernel, recurrent_latent)
    with ExitStack() as ctx:
        const = ctx.enter_context(tc.tile_pool(name="const", bufs=1))
        rawp = ctx.enter_context(tc.tile_pool(name="rawp", bufs=RAW_BUFS))
        grpp = ctx.enter_context(tc.tile_pool(name="grpp", bufs=GRP_BUFS))
        codp = ctx.enter_context(tc.tile_pool(name="codp", bufs=COD_BUFS))
        tmpp = ctx.enter_context(tc.tile_pool(name="tmpp", bufs=TMP_BUFS))
        psum = ctx.enter_context(tc.psum_pool(name="psum", bufs=1))
        ctx.enter_context(tc.manual_schedule())

        s_work = [[] for k in range(N_STREAM)]
        v_work = [[] for k in range(N_STREAM)]
        p_work = [[] for k in range(N_STREAM)]
        s_work[1] += [("act_copy", 1, 0), ("act_copy", 1, 1)]
        v_work[2] += [("act_quantise", 1, 0)]
        s_work[3] += [("act_copy", 2, 0), ("act_copy", 2, 1)]
        v_work[4] += [("act_quantise", 2, 0)]
        for gi in range(3):
            last = PASSES * gi + PASSES - 1
            for hh in range(2):
                first = last + 2 + (hh if gi < 2 else 0)
                if gi == 2 and hh == 1:
                    s_work[first].append(("c_transpose", 0, 0))
                s_work[first].append(("gate_act", gi, hh))
                if gi >= 1:
                    v_work[first + 1].append(("gate_mix", gi, hh))
                if gi == 2:
                    p_work[first + 1].append(("sum_c", gi, hh))
                    s_work[first + 2].append(("tanh_c", gi, hh))

        def split(s):
            shift = sum(SPLIT_SHIFT[w[0]] for w in s_work[s] + v_work[s]) + (SPLIT_SHIFT["pe_regroup"] if s in PE_UNITS else 0)
            cv = BASE_SPLIT + shift + (NO_QUANTISE_SHIFT if s == 0 else 0)
            return cv - cv % (2 * RUN)

        ident_f = const.tile([P, P], F32)
        make_identity(nc, ident_f[:])
        ident_b = const.tile([P, P], BF16)
        make_identity(nc, ident_b[:])
        warm = const.tile([P, 1], F32)
        nc.vector.memset(warm[:], 0.0)
        warm2 = const.tile([P, 1], F32)
        bias_rows = const.tile([P, P], BF16)
        nc.sync.dma_start(out=bias_rows[0:32, :], in_=bias.rearrange("(r c) -> r c", c=P))
        nc.vector.memset(bias_rows[32:64, :], 0.0)
        nc.vector.memset(bias_rows[64:128, :], 0.0)
        nc.scalar.activation(out=warm2[:], in_=warm[:], func=ACT.Tanh)

        units = [(g, c) for g in GATE_ORDER for c in range(PASSES)]
        raws = {}

        def load_unit(i):
            g, c = units[i]
            raw = rawp.tile([P, 4, U], BF16, name="raw")
            src = weights[c // 2][512 * (c % 2):512 * (c % 2) + 512, :].rearrange("(p j) n -> p j n", j=4)
            nc.sync.dma_start(out=raw[:], in_=src[:, :, U * g:U * g + U])
            raws[i] = raw

        def load_act(src, nm):
            t = const.tile([P, 2 * U], BF16, name=nm)
            nc.sync.dma_start(out=t[:], in_=src.rearrange("(p m) k -> p (m k)", m=2))
            return t

        x_sb = load_act(inputs, "x_sb")
        load_unit(0)
        load_unit(1)
        h_sb = load_act(h_tm1, "h_sb")
        load_unit(2)
        load_unit(3)
        z_sb = load_act(z_tm1, "z_sb")
        for i in range(4, RAW_BUFS):
            load_unit(i)
        acts = (x_sb, h_sb, z_sb)
        c_sb = {}

        b_ps = psum.tile([P, P], BF16, tag="b7", name="b_ps")
        nc.tensor.transpose(b_ps[:], bias_rows[:], ident_b[:])
        b32 = const.tile([P, 32], F32)
        nc.vector.tensor_copy(out=b32[:], in_=b_ps[:, 0:32])
        hb = const.tile([P, 32], F32)
        nc.vector.tensor_scalar(out=hb[:], in0=b32[:], scalar1=0.2, scalar2=0.5, op0=ALU.mult, op1=ALU.add)

        a_codes = const.tile([P, B + PASSES * B], U32, align_bytes=64)
        a_scales = const.tile([P, B + PASSES * B], U8, align_bytes=64)
        nc.vector.memset(a_codes[:, 0:B], 0)
        nc.vector.memset(a_scales[:, 0:B].bitcast(U32), 0)
        ga = [const.tile([P, 2 * 4 * B], BF16, align_bytes=64, name="ga%d" % s) for s in range(3)]
        state = const.tile([P, NJ, B], F32)
        th = const.tile([P, 2, U], F32)

        bank_free = [True] * 4 + [False] * 4
        a_ready = [False] * 3
        grouped = {}
        coded = {}
        acc = {}
        tmp_of = {}
        c_ps = {}
        reg_of = {}
        ct = {}
        pe_queue = [[] for b in range(NJ)]
        for i in range(N_UNITS):
            c = i % PASSES
            for j in range(NJ):
                pe_queue[bank_of(i // PASSES, j)].append((i, j ^ 1 if c == 0 and not alone(i // PASSES, j) else j))
        pe_head = [0] * NJ

        def half(j):
            return slice(B * (j % 2), B * (j % 2) + B)

        def flat(ap):
            return ap.rearrange("p j b -> p (j b)")

        def act_copy(s, gl, eng):
            a32 = acts[s][:].bitcast(F32)
            xt = psum.tile([P, 2, B], F32, tag="b%d" % (4 + (2 * s + gl) % 4), name="xt")
            for m in range(2):
                for u in range(2):
                    w0 = 512 * m + 256 * gl
                    nc.tensor.transpose(xt[:, u, P * m:P * m + P], a32[:, w0 + u:w0 + 256:2], ident_f[:])
            dst = ga[s][:].bitcast(F32)[:, 512 * gl:512 * gl + 512].rearrange("p (b u) -> p b u", u=2)
            srcv = xt[:].rearrange("p u b -> p b u")
            if eng == "v":
                nc.vector.tensor_copy(out=dst, in_=srcv)
            else:
                nc.scalar.copy(out=dst, in_=srcv)
            bank_free[4 + (2 * s + gl) % 4] = s > 0

        def act_quantise(s):
            cols = slice(B + 512 * s, B + 512 * s + 512)
            nc.vector.quantize_mx(out=a_codes[:, cols].bitcast(FP8X4), scales=a_scales[:, cols], in_=ga[s][:])
            a_ready[s] = True

        def regroup(i, cv):
            raw = raws[i]
            grp = grpp.tile([P, U, 4], BF16, align_bytes=64, name="grp")
            nc.vector.tensor_copy(out=grp[:, 0:cv, :].rearrange("p (c i) t -> p c t i", i=RUN),
                                  in_=raw[:, :, 0:cv].rearrange("p t (c i) -> p c t i", i=RUN))
            end = U - PE_COLS if i in PE_UNITS else U
            nc.scalar.copy(out=grp[:, cv:end, :].rearrange("p (c i) t -> p c t i", i=RUN),
                           in_=raw[:, :, cv:end].rearrange("p t (c i) -> p c t i", i=RUN))
            if i in PE_UNITS:
                nc.scalar.copy(out=grp[:, end:U, :].rearrange("p c t -> p (c t)"), in_=reg_of[i][:].rearrange("p c t -> p (c t)"))
                if i + 1 not in PE_UNITS:
                    bank_free[reg_bank(i)] = True
            grouped[i] = grp

        def reg_bank(i):
            return 7 if i // PASSES % 2 == 0 else 3

        def pe_regroup(i):
            bank_free[reg_bank(i)] = False
            reg = psum.tile([P, PE_COLS, 4], BF16, tag="b%d" % reg_bank(i), name="reg")
            for h in range(2):
                nc.tensor.matmul(reg[:, :, 2 * h:2 * h + 2].rearrange("p c t -> p t c"), lhsT=ident_b[:],
                                 rhs=raws[i][:, 2 * h:2 * h + 2, U - PE_COLS:U], start=True, stop=True)
            reg_of[i] = reg

        def quantise(i):
            codes = codp.tile([P, U], U32, align_bytes=64, name="codes")
            scales = codp.tile([P, U], U8, align_bytes=64, name="scales")
            nc.vector.quantize_mx(out=codes[:].bitcast(FP8X4), scales=scales[:],
                                  in_=grouped[i][:].rearrange("p w j -> p (w j)"))
            for j in range(NJ):
                coded[(i, j)] = (codes, scales, P * j)

        def ready(b):
            if pe_head[b] >= len(pe_queue[b]):
                return False
            i, j = pe_queue[b][pe_head[b]]
            c = i % PASSES
            return (i, j) in coded and a_ready[c // 2] and (c != 0 or bank_free[b] or j % 2 == 0 and not alone(i // PASSES, j))

        def multiply_what_is_ready():
            while True:
                cand = [pe_queue[b][pe_head[b]] + (b,) for b in range(NJ) if ready(b)]
                if not cand:
                    return
                i, j, b = min(cand)
                gi, c = divmod(i, PASSES)
                last = j % 2 == 1 or alone(gi, j)
                opens, closes = c == 0 and last, c == PASSES - 1 and last
                if opens:
                    acc[b] = psum.tile([P, 2 * B], F32, tag="b%d" % b, name="acc")
                    bank_free[b] = False
                codes, scales, w0 = coded[(i, j)]
                both = opens and not alone(gi, j)
                moving = slice(0, 2 * B) if both else slice(B + B * c, 2 * B + B * c)
                place = slice(0, 2 * B) if both else half(j)
                nc.tensor.matmul_mx(out=acc[b][:, place],
                                    lhsT=codes[:, w0:w0 + P].bitcast(FP8X4), lhsT_scale=scales[:, w0:w0 + P],
                                    rhs=a_codes[:, moving].bitcast(FP8X4), rhs_scale=a_scales[:, moving],
                                    start=opens, stop=closes)
                pe_head[b] += 1

        def gate_act(gi, hh):
            g = GATE_ORDER[gi]
            if gi > 0:
                tmp_of[(gi, hh)] = tmpp.tile([P, 4, B], F32, name="tmp")
            for jj in range(4):
                j = 4 * hh + jj
                if gi == 0:
                    nc.scalar.activation(out=state[:, j, :], in_=acc[bank_of(gi, j)][:, half(j)], func=ACT.Tanh,
                                         bias=b32[:, 8 * g + j:8 * g + j + 1], scale=1.0)
                else:
                    nc.scalar.activation(out=tmp_of[(gi, hh)][:, jj, :], in_=acc[bank_of(gi, j)][:, half(j)], func=ACT.Relu,
                                         bias=hb[:, 8 * g + j:8 * g + j + 1], scale=0.2)
                bank_free[bank_of(gi, j)] = gi < 2

        def gate_mix(gi, hh):
            js = slice(4 * hh, 4 * hh + 4)
            tmp = tmp_of[(gi, hh)]
            if gi == 2:
                nc.vector.scalar_tensor_tensor(out=flat(tmp[:]), in0=flat(tmp[:]), scalar=1.0,
                                               in1=flat(c_ps[hh][:]), op0=ALU.min, op1=ALU.mult)
            else:
                st = flat(state[:, js, :])
                nc.vector.scalar_tensor_tensor(out=st, in0=flat(tmp[:]), scalar=1.0, in1=st,
                                               op0=ALU.min, op1=ALU.mult)

        def sum_c(hh):
            for m in range(2):
                ct[(hh, m)] = psum.tile([P, 512], F32, tag="b%d" % (2 - 2 * hh + m), name="ct")
                for jj in range(4):
                    dst = ct[(hh, m)][:, P * jj:P * jj + P]
                    nc.tensor.matmul(dst, lhsT=state[:, 4 * hh + jj, P * m:P * m + P], rhs=ident_f[:],
                                     is_transpose=True, start=True, stop=False)
                    nc.tensor.matmul(dst, lhsT=tmp_of[(2, hh)][:, jj, P * m:P * m + P], rhs=ident_f[:],
                                     is_transpose=True, start=False, stop=True)

        def tanh_c(hh):
            for m in range(2):
                nc.scalar.activation(out=th[:, m, 512 * hh:512 * hh + 512], in_=ct[(hh, m)][:], func=ACT.Tanh)
            if hh == 1:
                bank_free[0] = True

        def c_transpose():
            for hh in range(2):
                c_ps[hh] = psum.tile([P, 4, B], BF16, tag="b%d" % hh, name="c_ps")
                for jj in range(4):
                    for m in range(2):
                        col = U * m + P * (4 * hh + jj)
                        nc.tensor.transpose(c_ps[hh][:, jj, P * m:P * m + P], c_sb[0][:, col:col + P], ident_b[:])

        def do(w):
            kind, a, b = w
            if kind == "act_copy":
                act_copy(a, b, "s")
            elif kind == "act_quantise":
                act_quantise(a)
            elif kind == "gate_act":
                gate_act(a, b)
            elif kind == "gate_mix":
                gate_mix(a, b)
            elif kind == "sum_c":
                sum_c(b)
            elif kind == "tanh_c":
                tanh_c(b)
            elif kind == "c_transpose":
                c_transpose()

        act_copy(0, 0, "v")
        act_copy(0, 1, "s")
        act_quantise(0)

        next_load = [RAW_BUFS]
        for s in range(N_STREAM):
            regroup(s, split(s))
            if next_load[0] < N_UNITS:
                load_unit(next_load[0])
                if next_load[0] == C_AFTER:
                    c_sb[0] = load_act(c_tm1, "c_sb")
                next_load[0] += 1
            if s >= 1:
                quantise(s - 1)
            for w in s_work[s]:
                do(w)
            for w in v_work[s]:
                do(w)
            if s + 1 in PE_UNITS:
                pe_regroup(s + 1)
            multiply_what_is_ready()
            for w in p_work[s]:
                do(w)

        out_v = out.rearrange("(p m) u -> p m u", m=2)
        blk = {}
        hp = {}

        def block_regroup(q):
            grp = grpp.tile([P, U, 4], BF16, align_bytes=64, name="grp")
            j0, nj = BLOCKS[q]
            bw = P * nj
            cols = slice(P * j0, P * j0 + bw)
            nc.vector.tensor_copy(out=grp[:, 0:bw, :].rearrange("p (c i) t -> p c t i", i=RUN),
                                  in_=raws[N_STREAM][:, :, cols].rearrange("p t (c i) -> p c t i", i=RUN))
            nc.scalar.copy(out=grp[:, bw:2 * bw, :].rearrange("p (c i) t -> p c t i", i=RUN),
                           in_=raws[N_STREAM + 1][:, :, cols].rearrange("p t (c i) -> p c t i", i=RUN))
            blk[q] = grp

        def block_multiply(q):
            codes = codp.tile([P, U], U32, align_bytes=64, name="codes")
            scales = codp.tile([P, U], U8, align_bytes=64, name="scales")
            j0, nj = BLOCKS[q]
            bw = P * nj
            nc.vector.quantize_mx(out=codes[:, 0:2 * bw].bitcast(FP8X4), scales=scales[:, 0:2 * bw],
                                  in_=blk[q][:, 0:2 * bw, :].rearrange("p w j -> p (w j)"))
            for cc in range(2):
                for jj in range(nj):
                    coded[(N_STREAM + cc, j0 + jj)] = (codes, scales, bw * cc + P * jj)
            multiply_what_is_ready()

        def block_act(q):
            g = GATE_ORDER[3]
            tmp = tmpp.tile([P, 4, B], F32, name="tmp")
            j0, nj = BLOCKS[q]
            for jj in range(nj):
                j = j0 + jj
                nc.scalar.activation(out=tmp[:, jj, :], in_=acc[bank_of(3, j)][:, half(j)], func=ACT.Relu,
                                     bias=hb[:, 8 * g + j:8 * g + j + 1], scale=0.2)
            hp[q] = psum.tile([P, 2, P * nj], F32, tag="b%d" % bank_of(3, j0), name="hp")
            for m in range(2):
                for jj in range(nj):
                    nc.tensor.transpose(hp[q][:, m, P * jj:P * jj + P], tmp[:, jj, P * m:P * m + P], ident_f[:])

        def block_finish(q):
            j0, nj = BLOCKS[q]
            dst = th[:, :, P * j0:P * (j0 + nj)]
            nc.vector.scalar_tensor_tensor(out=dst, in0=hp[q][:], scalar=1.0, in1=dst,
                                           op0=ALU.min, op1=ALU.mult)
            nc.sync.dma_start(out=out_v[:, :, P * j0:P * (j0 + nj)], in_=dst)

        nb = len(BLOCKS)
        for step in range(nb + 3):
            if step < nb:
                block_regroup(step)
            if step == 0:
                quantise(N_STREAM - 1)
                multiply_what_is_ready()
            if 1 <= step < nb + 1:
                block_multiply(step - 1)
            if 2 <= step < nb + 2:
                block_act(step - 2)
            if step >= 3:
                block_finish(step - 3)
